import numpy as np
import ml_dtypes


def mxq(x, axis, fmt="e4m3"):
    dtype, down = {"e4m3": (ml_dtypes.float8_e4m3fn, 7), "e5m2": (ml_dtypes.float8_e5m2, 14)}[fmt]
    v = np.moveaxis(np.asarray(x, np.float32).astype(ml_dtypes.bfloat16).astype(np.float64), axis, -1)
    blocks = v.reshape(v.shape[:-1] + (-1, 32))
    amax = np.abs(blocks).max(-1, keepdims=True)
    byte = np.maximum(np.where(amax > 0, np.frexp(amax)[1] - 1 + 127, 0) - down, 1)
    scale = np.exp2(byte - 127.0)
    codes = (blocks / scale).astype(np.float32).astype(dtype).astype(np.float64)
    return np.moveaxis((codes * scale).reshape(v.shape), -1, axis)


WIDE = False


def mx_kscale(k):
    if not WIDE:
        return np.ones(k)
    levels = np.array([10, -10, 5, -5, 0])
    a = np.random.permutation(np.resize(levels, k // 512 * 4)).reshape(k // 512, 4)
    idx = np.arange(k)
    return np.exp2(a[idx // 512, idx % 128 // 32])


BF16 = ml_dtypes.bfloat16


def bf(x):
    return np.asarray(x, np.float32).astype(BF16)


def f64(x):
    return np.asarray(x).astype(np.float64)


B, S, D, NH, NKV, HD = 2, 256, 2048, 16, 4, 128
EPS = 1e-6
QS = NH * HD
KS = NKV * HD
E = QS + KS + KS
HP = HD // 2


def rmsnorm(v, w):
    ms = np.mean(np.square(v), axis=-1, keepdims=True)
    return v * (1.0 / np.sqrt(ms + EPS)) * w


def apply_rotary_emb(v, fc):
    vs = v.reshape(*v.shape[:-1], HP, 2)
    f = fc[None, :, None, :, :]
    vr, vi = vs[..., 0], vs[..., 1]
    fr, fi = f[..., 0], f[..., 1]
    return np.stack([vr * fr - vi * fi, vi * fr + vr * fi], axis=-1).reshape(v.shape)


def setup_inputs():
    s = mx_kscale(D)
    return {"x": bf(np.random.standard_normal((B, S, D)) * s),
            "freqs_cis": bf(np.random.standard_normal((S, HP, 2))),
            "wqkv": bf(np.random.standard_normal((E, D)) / np.sqrt(D) / s[None, :]),
            "q_norm_w": bf(1.0 + 0.1 * np.random.standard_normal(HD)),
            "k_norm_w": bf(1.0 + 0.1 * np.random.standard_normal(HD))}


def reference(x, freqs_cis, wqkv, q_norm_w, k_norm_w):
    fc = f64(freqs_cis)
    qkv = mxq(f64(x), 2, "e4m3") @ mxq(f64(wqkv), 1, "e4m3").T
    q = qkv[..., :QS].reshape(B, S, NH, HD)
    k = qkv[..., QS:QS + KS].reshape(B, S, NKV, HD)
    v = qkv[..., QS + KS:].reshape(B, S, NKV, HD)
    q = rmsnorm(q, f64(q_norm_w))
    k = rmsnorm(k, f64(k_norm_w))
    q_rot = apply_rotary_emb(q, fc)
    k_rot = apply_rotary_emb(k, fc)
    return q_rot, k_rot, v

@@ -1,0 +1,273 @@
+from contextlib import ExitStack
+
+import concourse.mybir as mybir
+from concourse.masks import make_identity
+
+F32 = mybir.dt.float32
+BF16 = mybir.dt.bfloat16
+U32 = mybir.dt.uint32
+U8 = mybir.dt.uint8
+FP8X4 = mybir.dt.float8_e4m3fn_x4
+ALU = mybir.AluOpType
+ACT = mybir.ActivationFunctionType
+
+P = 128
+PACK = 4
+K_PASS = P * PACK
+WORDS_PASS = K_PASS // 2
+
+TOKENS = 512
+D = 2048
+PASSES = D // K_PASS
+TOKEN_TILES = TOKENS // P
+HD = 128
+HP = HD // 2
+GROUP = 512
+HALF = GROUP // 2
+Q_GROUPS = 4
+K_GROUP = 4
+V_GROUP = 5
+N_GROUPS = 6
+W_BUFS = 3
+EPS = 1e-6
+
+FLOPS = 2 * TOKENS * D * (N_GROUPS * GROUP)
+
+
+def tile_attention_pa_kernel(tc, x, freqs_cis, wqkv, q_norm_w, k_norm_w, out_0, out_1, out_2):
+    nc = tc.nc
+    with ExitStack() as ctx:
+        const = ctx.enter_context(tc.tile_pool(name="const", bufs=1))
+        w_pool = ctx.enter_context(tc.tile_pool(name="w_pool", bufs=W_BUFS))
+        stage = ctx.enter_context(tc.tile_pool(name="stage", bufs=4))
+        quantised = ctx.enter_context(tc.tile_pool(name="quantised", bufs=2))
+        work = ctx.enter_context(tc.tile_pool(name="work", bufs=3))
+        small = ctx.enter_context(tc.tile_pool(name="small", bufs=4))
+        t_psum = ctx.enter_context(tc.psum_pool(name="t_psum", bufs=4))
+        acc_psum = ctx.enter_context(tc.psum_pool(name="acc_psum", bufs=4))
+
+        x_rows_dram = x.rearrange("b s k -> (b s) k")
+        out_dram = [
+            out_0.rearrange("b s h d -> (b s) (h d)"),
+            out_1.rearrange("b s h d -> (b s) (h d)"),
+            out_2.rearrange("b s h d -> (b s) (h d)"),
+        ]
+
+        freqs = const.tile([P, 2, HP, 2], BF16, name="freqs")
+        nc.scalar.dma_start(out=freqs[:], in_=freqs_cis.rearrange("(a p) j t -> p a j t", p=P))
+        gain_row = const.tile([P, 2, HD], BF16, name="gain_row")
+        nc.vector.memset(gain_row[:], 0.0)
+        nc.scalar.dma_start(out=gain_row[0:1, 0, :], in_=q_norm_w.unsqueeze(0))
+        nc.scalar.dma_start(out=gain_row[0:1, 1, :], in_=k_norm_w.unsqueeze(0))
+
+        x_rows = const.tile([P, TOKEN_TILES, D], BF16, name="x_rows")
+        for m in range(TOKEN_TILES):
+            nc.sync.dma_start(out=x_rows[:, m, :], in_=x_rows_dram[P * m : P * (m + 1), :])
+
+        w_rows = {}
+
+        def load_w(g):
+            w_rows[g] = w_pool.tile([P, 2, 2, D], BF16, name="w_rows")
+            for b in range(2):
+                first = GROUP * g + HALF * b
+                nc.sync.dma_start(
+                    out=w_rows[g][:, b, :, :].rearrange("p e k -> p (e k)"),
+                    in_=wqkv[first : first + HALF, :].rearrange("(p e) k -> p (e k)", e=2),
+                )
+
+        for g in range(W_BUFS):
+            load_w(g)
+
+        eps = const.tile([P, 1], F32, name="eps")
+        nc.vector.memset(eps[:], EPS)
+        warm = const.tile([P, 1], F32, name="warm")
+        nc.scalar.activation(out=warm[:], in_=eps[:], func=ACT.Sqrt)
+        ones = const.tile([P, P], BF16, name="ones")
+        nc.vector.memset(ones[:], 1.0)
+        ident = const.tile([P, P], F32, name="ident")
+        make_identity(nc, ident[:])
+
+        def transpose_pass(row_tiles, c, vector_helps):
+            grouped = stage.tile([P, GROUP, PACK], BF16, align_bytes=64, name="grouped")
+            grouped_words = grouped[:].bitcast(F32)
+            for b in range(2):
+                bank = t_psum.tile([P, 2, HALF], F32, name="bank")
+                for u in range(2):
+                    for i in range(2):
+                        words = row_tiles[2 * b + i].bitcast(F32)
+                        first = WORDS_PASS * c + P * u
+                        nc.tensor.transpose(
+                            out=bank[:, u, P * i : P * (i + 1)],
+                            in_=words[:, first : first + P],
+                            identity=ident[:],
+                        )
+                dst = grouped_words[:, HALF * b : HALF * (b + 1), :]
+                src = bank[:].rearrange("p u n -> p n u")
+                if vector_helps and b == 1:
+                    nc.vector.tensor_copy(out=dst, in_=src)
+                else:
+                    nc.scalar.copy(out=dst, in_=src)
+            return grouped
+
+        def quantise(grouped, codes, scales, c):
+            nc.vector.quantize_mx(
+                out=codes[:, c, :].bitcast(FP8X4),
+                scales=scales[:, c, :],
+                in_=grouped[:].rearrange("p n t -> p (n t)"),
+            )
+
+        def w_row_tiles(g):
+            return [w_rows[g][:, b, e, :] for b in range(2) for e in range(2)]
+
+        def new_w_operand():
+            codes = quantised.tile([P, PASSES, GROUP], U32, align_bytes=64, name="w_codes")
+            scales = quantised.tile([P, PASSES, GROUP], U8, align_bytes=64, name="w_scales")
+            return codes, scales
+
+        x_codes = const.tile([P, PASSES, TOKENS], U32, align_bytes=64, name="x_codes")
+        x_scales = const.tile([P, PASSES, TOKENS], U8, align_bytes=64, name="x_scales")
+        x_tiles = [x_rows[:, m, :] for m in range(TOKEN_TILES)]
+        w_operand = {0: new_w_operand()}
+
+        head = [(x_tiles, c, x_codes, x_scales) for c in range(PASSES)]
+        head = head + [(w_row_tiles(0), c, w_operand[0][0], w_operand[0][1]) for c in range(PASSES)]
+        head_grouped = []
+        for n in range(len(head)):
+            head_grouped.append(transpose_pass(head[n][0], head[n][1], True))
+            if n >= 1:
+                quantise(head_grouped[n - 1], head[n - 1][2], head[n - 1][3], head[n - 1][1])
+            if n == PASSES - 1:
+                gain_bank = t_psum.tile([P, 2, HALF], F32, name="bank")
+                nc.tensor.matmul(
+                    out=gain_bank[:, 0, :],
+                    lhsT=ones[:],
+                    rhs=gain_row[:].rearrange("p a d -> p (a d)"),
+                    start=True,
+                    stop=True,
+                )
+                gains = const.tile([P, 2, HP, 2], F32, name="gains")
+                nc.scalar.copy(out=gains[:].rearrange("p a j e -> p (a j e)"), in_=gain_bank[:, 0, :])
+        last = len(head) - 1
+        quantise(head_grouped[last], head[last][2], head[last][3], head[last][1])
+
+        same = {}
+        cross = {}
+        for kind in range(2):
+            for a in range(2):
+                same_t = const.tile([P, 2, 2, HP], F32, name="same%d%d" % (kind, a))
+                cross_t = const.tile([P, 2, HP], F32, name="cross%d%d" % (kind, a))
+                for h in range(2):
+                    nc.vector.tensor_tensor(
+                        out=same_t[:, :, h, :],
+                        in0=gains[:, kind, :, :].rearrange("p j e -> p e j"),
+                        in1=freqs[:, a, :, 0].unsqueeze(1).to_broadcast([P, 2, HP]),
+                        op=ALU.mult,
+                    )
+                nc.vector.scalar_tensor_tensor(
+                    out=cross_t[:, 0, :],
+                    in0=gains[:, kind, :, 1],
+                    scalar=-1.0,
+                    in1=freqs[:, a, :, 1],
+                    op0=ALU.mult,
+                    op1=ALU.mult,
+                )
+                nc.vector.tensor_tensor(
+                    out=cross_t[:, 1, :], in0=gains[:, kind, :, 0], in1=freqs[:, a, :, 1], op=ALU.mult
+                )
+                same[(kind, a)] = same_t
+                cross[(kind, a)] = cross_t
+
+        def multiply(g, m):
+            acc = acc_psum.tile([P, 2, 2, 2, HP], F32, name="acc")
+            codes, scales = w_operand[g]
+            for c in range(PASSES):
+                nc.tensor.matmul_mx(
+                    out=acc[:].rearrange("p b e h j -> p (b e h j)"),
+                    lhsT=x_codes[:, c, P * m : P * (m + 1)].bitcast(FP8X4),
+                    lhsT_scale=x_scales[:, c, P * m : P * (m + 1)],
+                    rhs=codes[:, c, :].bitcast(FP8X4),
+                    rhs_scale=scales[:, c, :],
+                    start=(c == 0),
+                    stop=(c == PASSES - 1),
+                )
+            return acc
+
+        def store(g, m, result):
+            if g < Q_GROUPS:
+                dst = out_dram[0][P * m : P * (m + 1), GROUP * g : GROUP * (g + 1)]
+            elif g == K_GROUP:
+                dst = out_dram[1][P * m : P * (m + 1), :]
+            else:
+                dst = out_dram[2][P * m : P * (m + 1), :]
+            nc.sync.dma_start(out=dst, in_=result[:].rearrange("p b h j e -> p (b h j e)"))
+
+        def norm_and_rotate(g, m, acc):
+            kind = 0 if g < Q_GROUPS else 1
+            same_t = same[(kind, m % 2)]
+            cross_t = cross[(kind, m % 2)]
+            sumsq = small.tile([P, 2, 2], F32, name="sumsq")
+            for b in range(2):
+                for h in range(2):
+                    squares = small.tile([P, 2, HP], BF16, name="squares")
+                    nc.scalar.activation(
+                        out=squares[:], in_=acc[:, b, :, h, :], func=ACT.Square, accum_out=sumsq[:, b, h : h + 1]
+                    )
+            rms = small.tile([P, 2, 2], F32, name="rms")
+            nc.scalar.activation(out=rms[:], in_=sumsq[:], func=ACT.Sqrt, bias=eps[:, 0:1], scale=1.0 / HD)
+            inv = small.tile([P, 2, 2], F32, name="inv")
+            nc.vector.reciprocal(out=inv[:], in_=rms[:])
+
+            t_same = work.tile([P, 2, 2, 2, HP], F32, name="t_same")
+            nc.vector.tensor_tensor(
+                out=t_same[:].rearrange("p b e h j -> p b (e h j)"),
+                in0=acc[:].rearrange("p b e h j -> p b (e h j)"),
+                in1=same_t[:].rearrange("p e h j -> p (e h j)").unsqueeze(1).to_broadcast([P, 2, HALF]),
+                op=ALU.mult,
+            )
+            t_cross = work.tile([P, 2, 2, 2, HP], F32, name="t_cross")
+            for b in range(2):
+                for h in range(2):
+                    for e in range(2):
+                        nc.vector.scalar_tensor_tensor(
+                            out=t_cross[:, b, e, h, :],
+                            in0=acc[:, b, 1 - e, h, :],
+                            scalar=inv[:, b, h : h + 1],
+                            in1=cross_t[:, e, :],
+                            op0=ALU.mult,
+                            op1=ALU.mult,
+                        )
+            result = work.tile([P, 2, 2, HP, 2], F32, name="result")
+            for b in range(2):
+                for h in range(2):
+                    nc.vector.scalar_tensor_tensor(
+                        out=result[:, b, h, :, :],
+                        in0=t_same[:, b, :, h, :].rearrange("p e j -> p j e"),
+                        scalar=inv[:, b, h : h + 1],
+                        in1=t_cross[:, b, :, h, :].rearrange("p e j -> p j e"),
+                        op0=ALU.mult,
+                        op1=ALU.add,
+                    )
+            store(g, m, result)
+
+        def copy_out(g, m, acc):
+            result = work.tile([P, 2, 2, HP, 2], F32, name="result")
+            nc.scalar.copy(
+                out=result[:].rearrange("p b h j e -> p b (h j) e"),
+                in_=acc[:].rearrange("p b e h j -> p b (h j) e"),
+            )
+            store(g, m, result)
+
+        for g in range(N_GROUPS):
+            if g + W_BUFS < N_GROUPS:
+                load_w(g + W_BUFS)
+            if g + 1 < N_GROUPS:
+                w_operand[g + 1] = new_w_operand()
+            for i in range(TOKEN_TILES):
+                if g + 1 < N_GROUPS:
+                    grouped = transpose_pass(w_row_tiles(g + 1), i, False)
+                    quantise(grouped, w_operand[g + 1][0], w_operand[g + 1][1], i)
+                acc = multiply(g, i)
+                if g == V_GROUP:
+                    copy_out(g, i, acc)
+                else:
+                    norm_and_rotate(g, i, acc)

@@ -46,6 +46,8 @@ def tile_attention_pa_kernel(tc, x, freqs_cis, wqkv, q_norm_w, k_norm_w, out_0, 
         t_psum = ctx.enter_context(tc.psum_pool(name="t_psum", bufs=4))
         acc_psum = ctx.enter_context(tc.psum_pool(name="acc_psum", bufs=4))
 
+        ctx.enter_context(tc.manual_schedule())
+
         x_rows_dram = x.rearrange("b s k -> (b s) k")
         out_dram = [
             out_0.rearrange("b s h d -> (b s) (h d)"),

@@ -39,9 +39,9 @@ def tile_attention_pa_kernel(tc, x, freqs_cis, wqkv, q_norm_w, k_norm_w, out_0, 
     with ExitStack() as ctx:
         const = ctx.enter_context(tc.tile_pool(name="const", bufs=1))
         w_pool = ctx.enter_context(tc.tile_pool(name="w_pool", bufs=W_BUFS))
-        stage = ctx.enter_context(tc.tile_pool(name="stage", bufs=4))
+        stage = ctx.enter_context(tc.tile_pool(name="stage", bufs=6))
         quantised = ctx.enter_context(tc.tile_pool(name="quantised", bufs=2))
-        work = ctx.enter_context(tc.tile_pool(name="work", bufs=3))
+        work = ctx.enter_context(tc.tile_pool(name="work", bufs=4))
         small = ctx.enter_context(tc.tile_pool(name="small", bufs=4))
         t_psum = ctx.enter_context(tc.psum_pool(name="t_psum", bufs=4))
         acc_psum = ctx.enter_context(tc.psum_pool(name="acc_psum", bufs=4))
@@ -63,7 +63,8 @@ def tile_attention_pa_kernel(tc, x, freqs_cis, wqkv, q_norm_w, k_norm_w, out_0, 
         nc.scalar.dma_start(out=gain_row[0:1, 1, :], in_=k_norm_w.unsqueeze(0))
 
         x_rows = const.tile([P, TOKEN_TILES, D], BF16, name="x_rows")
-        for m in range(TOKEN_TILES):
+
+        def load_x(m):
             nc.sync.dma_start(out=x_rows[:, m, :], in_=x_rows_dram[P * m : P * (m + 1), :])
 
         w_rows = {}
@@ -77,7 +78,11 @@ def tile_attention_pa_kernel(tc, x, freqs_cis, wqkv, q_norm_w, k_norm_w, out_0, 
                     in_=wqkv[first : first + HALF, :].rearrange("(p e) k -> p (e k)", e=2),
                 )
 
-        for g in range(W_BUFS):
+        load_x(0)
+        load_w(0)
+        for m in range(1, TOKEN_TILES):
+            load_x(m)
+        for g in range(1, W_BUFS):
             load_w(g)
 
         eps = const.tile([P, 1], F32, name="eps")
@@ -89,82 +94,85 @@ def tile_attention_pa_kernel(tc, x, freqs_cis, wqkv, q_norm_w, k_norm_w, out_0, 
         ident = const.tile([P, P], F32, name="ident")
         make_identity(nc, ident[:])
 
-        def transpose_pass(row_tiles, c, vector_helps):
-            grouped = stage.tile([P, GROUP, PACK], BF16, align_bytes=64, name="grouped")
-            grouped_words = grouped[:].bitcast(F32)
-            for b in range(2):
-                bank = t_psum.tile([P, 2, HALF], F32, name="bank")
-                for u in range(2):
-                    for i in range(2):
-                        words = row_tiles[2 * b + i].bitcast(F32)
-                        first = WORDS_PASS * c + P * u
-                        nc.tensor.transpose(
-                            out=bank[:, u, P * i : P * (i + 1)],
-                            in_=words[:, first : first + P],
-                            identity=ident[:],
-                        )
-                dst = grouped_words[:, HALF * b : HALF * (b + 1), :]
-                src = bank[:].rearrange("p u n -> p n u")
-                if vector_helps and b == 1:
-                    nc.vector.tensor_copy(out=dst, in_=src)
-                else:
-                    nc.scalar.copy(out=dst, in_=src)
-            return grouped
+        def new_grouped():
+            return stage.tile([P, GROUP, PACK], BF16, align_bytes=64, name="grouped")
 
-        def quantise(grouped, codes, scales, c):
+        def transpose_half(grouped, b, pieces, on_vector):
+            bank = t_psum.tile([P, 2, HALF], F32, name="bank")
+            for u in range(2):
+                for i in range(2):
+                    rows, c = pieces[i]
+                    first = WORDS_PASS * c + P * u
+                    nc.tensor.transpose(
+                        out=bank[:, u, P * i : P * (i + 1)],
+                        in_=rows.bitcast(F32)[:, first : first + P],
+                        identity=ident[:],
+                    )
+            dst = grouped[:].bitcast(F32)[:, HALF * b : HALF * (b + 1), :]
+            src = bank[:].rearrange("p u n -> p n u")
+            if on_vector:
+                nc.vector.tensor_copy(out=dst, in_=src)
+            else:
+                nc.scalar.copy(out=dst, in_=src)
+
+        def w_pieces(g, b, c):
+            return [(w_rows[g][:, b, e, :], c) for e in range(2)]
+
+        def x_pieces(m, b):
+            return [(x_rows[:, m, :], 2 * b + i) for i in range(2)]
+
+        def quantise(grouped, codes, scales):
             nc.vector.quantize_mx(
-                out=codes[:, c, :].bitcast(FP8X4),
-                scales=scales[:, c, :],
-                in_=grouped[:].rearrange("p n t -> p (n t)"),
+                out=codes.bitcast(FP8X4), scales=scales, in_=grouped[:].rearrange("p n t -> p (n t)")
             )
-
-        def w_row_tiles(g):
-            return [w_rows[g][:, b, e, :] for b in range(2) for e in range(2)]
 
         def new_w_operand():
             codes = quantised.tile([P, PASSES, GROUP], U32, align_bytes=64, name="w_codes")
             scales = quantised.tile([P, PASSES, GROUP], U8, align_bytes=64, name="w_scales")
             return codes, scales
 
-        x_codes = const.tile([P, PASSES, TOKENS], U32, align_bytes=64, name="x_codes")
-        x_scales = const.tile([P, PASSES, TOKENS], U8, align_bytes=64, name="x_scales")
-        x_tiles = [x_rows[:, m, :] for m in range(TOKEN_TILES)]
-        w_operand = {0: new_w_operand()}
+        x_codes = const.tile([P, TOKEN_TILES, PASSES * P], U32, align_bytes=64, name="x_codes")
+        x_scales = const.tile([P, TOKEN_TILES, PASSES * P], U8, align_bytes=64, name="x_scales")
 
-        head = [(x_tiles, c, x_codes, x_scales) for c in range(PASSES)]
-        head = head + [(w_row_tiles(0), c, w_operand[0][0], w_operand[0][1]) for c in range(PASSES)]
-        head_grouped = []
-        for n in range(len(head)):
-            head_grouped.append(transpose_pass(head[n][0], head[n][1], True))
-            if n >= 1:
-                quantise(head_grouped[n - 1], head[n - 1][2], head[n - 1][3], head[n - 1][1])
-            if n == PASSES - 1:
-                gain_bank = t_psum.tile([P, 2, HALF], F32, name="bank")
-                nc.tensor.matmul(
-                    out=gain_bank[:, 0, :],
-                    lhsT=ones[:],
-                    rhs=gain_row[:].rearrange("p a d -> p (a d)"),
-                    start=True,
-                    stop=True,
-                )
-                gains = const.tile([P, 2, HP, 2], F32, name="gains")
-                nc.scalar.copy(out=gains[:].rearrange("p a j e -> p (a j e)"), in_=gain_bank[:, 0, :])
-        last = len(head) - 1
-        quantise(head_grouped[last], head[last][2], head[last][3], head[last][1])
+        def prepare_x(m):
+            grouped = new_grouped()
+            for b in range(2):
+                transpose_half(grouped, b, x_pieces(m, b), b == 1)
+            return grouped
+
+        def quantise_x(m, grouped):
+            quantise(grouped, x_codes[:, m, :], x_scales[:, m, :])
+
+        w_operand = {0: new_w_operand()}
+        x_grouped = prepare_x(0)
+        first_grouped = [new_grouped() for c in range(PASSES)]
+        for c in range(PASSES):
+            transpose_half(first_grouped[c], 0, w_pieces(0, 0, c), c % 2 == 1)
+        quantise_x(0, x_grouped)
+
+        gain_bank = t_psum.tile([P, 2, HALF], F32, name="bank")
+        nc.tensor.matmul(
+            out=gain_bank[:, 0, :],
+            lhsT=ones[:],
+            rhs=gain_row[:].rearrange("p a d -> p (a d)"),
+            start=True,
+            stop=True,
+        )
+        gains = const.tile([P, 2, HP, 2], F32, name="gains")
+        nc.scalar.copy(out=gains[:].rearrange("p a j e -> p (a j e)"), in_=gain_bank[:, 0, :])
 
         same = {}
         cross = {}
         for kind in range(2):
             for a in range(2):
-                same_t = const.tile([P, 2, 2, HP], F32, name="same%d%d" % (kind, a))
+                same_t = const.tile([P, 2, HP], F32, name="same%d%d" % (kind, a))
                 cross_t = const.tile([P, 2, HP], F32, name="cross%d%d" % (kind, a))
-                for h in range(2):
-                    nc.vector.tensor_tensor(
-                        out=same_t[:, :, h, :],
-                        in0=gains[:, kind, :, :].rearrange("p j e -> p e j"),
-                        in1=freqs[:, a, :, 0].unsqueeze(1).to_broadcast([P, 2, HP]),
-                        op=ALU.mult,
-                    )
+                nc.vector.tensor_tensor(
+                    out=same_t[:],
+                    in0=gains[:, kind, :, :].rearrange("p j e -> p e j"),
+                    in1=freqs[:, a, :, 0].unsqueeze(1).to_broadcast([P, 2, HP]),
+                    op=ALU.mult,
+                )
                 nc.vector.scalar_tensor_tensor(
                     out=cross_t[:, 0, :],
                     in0=gains[:, kind, :, 1],
@@ -179,14 +187,20 @@ def tile_attention_pa_kernel(tc, x, freqs_cis, wqkv, q_norm_w, k_norm_w, out_0, 
                 same[(kind, a)] = same_t
                 cross[(kind, a)] = cross_t
 
+        for c in range(PASSES):
+            transpose_half(first_grouped[c], 1, w_pieces(0, 1, c), c % 2 == 1)
+            if c >= 1:
+                quantise(first_grouped[c - 1], w_operand[0][0][:, c - 1, :], w_operand[0][1][:, c - 1, :])
+        quantise(first_grouped[PASSES - 1], w_operand[0][0][:, PASSES - 1, :], w_operand[0][1][:, PASSES - 1, :])
+
         def multiply(g, m):
             acc = acc_psum.tile([P, 2, 2, 2, HP], F32, name="acc")
             codes, scales = w_operand[g]
             for c in range(PASSES):
                 nc.tensor.matmul_mx(
                     out=acc[:].rearrange("p b e h j -> p (b e h j)"),
-                    lhsT=x_codes[:, c, P * m : P * (m + 1)].bitcast(FP8X4),
-                    lhsT_scale=x_scales[:, c, P * m : P * (m + 1)],
+                    lhsT=x_codes[:, m, P * c : P * (c + 1)].bitcast(FP8X4),
+                    lhsT_scale=x_scales[:, m, P * c : P * (c + 1)],
                     rhs=codes[:, c, :].bitcast(FP8X4),
                     rhs_scale=scales[:, c, :],
                     start=(c == 0),
@@ -203,10 +217,7 @@ def tile_attention_pa_kernel(tc, x, freqs_cis, wqkv, q_norm_w, k_norm_w, out_0, 
                 dst = out_dram[2][P * m : P * (m + 1), :]
             nc.sync.dma_start(out=dst, in_=result[:].rearrange("p b h j e -> p (b h j e)"))
 
-        def norm_and_rotate(g, m, acc):
-            kind = 0 if g < Q_GROUPS else 1
-            same_t = same[(kind, m % 2)]
-            cross_t = cross[(kind, m % 2)]
+        def norms(acc):
             sumsq = small.tile([P, 2, 2], F32, name="sumsq")
             for b in range(2):
                 for h in range(2):
@@ -218,20 +229,27 @@ def tile_attention_pa_kernel(tc, x, freqs_cis, wqkv, q_norm_w, k_norm_w, out_0, 
             nc.scalar.activation(out=rms[:], in_=sumsq[:], func=ACT.Sqrt, bias=eps[:, 0:1], scale=1.0 / HD)
             inv = small.tile([P, 2, 2], F32, name="inv")
             nc.vector.reciprocal(out=inv[:], in_=rms[:])
+            return inv
 
+        def rotate(g, m, acc, inv):
+            kind = 0 if g < Q_GROUPS else 1
+            same_t = same[(kind, m % 2)]
+            cross_t = cross[(kind, m % 2)]
             t_same = work.tile([P, 2, 2, 2, HP], F32, name="t_same")
-            nc.vector.tensor_tensor(
-                out=t_same[:].rearrange("p b e h j -> p b (e h j)"),
-                in0=acc[:].rearrange("p b e h j -> p b (e h j)"),
-                in1=same_t[:].rearrange("p e h j -> p (e h j)").unsqueeze(1).to_broadcast([P, 2, HALF]),
-                op=ALU.mult,
-            )
             t_cross = work.tile([P, 2, 2, 2, HP], F32, name="t_cross")
             for b in range(2):
                 for h in range(2):
+                    nc.vector.scalar_tensor_tensor(
+                        out=t_same[:, b, h, :, :],
+                        in0=acc[:, b, :, h, :],
+                        scalar=inv[:, b, h : h + 1],
+                        in1=same_t[:],
+                        op0=ALU.mult,
+                        op1=ALU.mult,
+                    )
                     for e in range(2):
                         nc.vector.scalar_tensor_tensor(
-                            out=t_cross[:, b, e, h, :],
+                            out=t_cross[:, b, h, e, :],
                             in0=acc[:, b, 1 - e, h, :],
                             scalar=inv[:, b, h : h + 1],
                             in1=cross_t[:, e, :],
@@ -240,15 +258,12 @@ def tile_attention_pa_kernel(tc, x, freqs_cis, wqkv, q_norm_w, k_norm_w, out_0, 
                         )
             result = work.tile([P, 2, 2, HP, 2], F32, name="result")
             for b in range(2):
-                for h in range(2):
-                    nc.vector.scalar_tensor_tensor(
-                        out=result[:, b, h, :, :],
-                        in0=t_same[:, b, :, h, :].rearrange("p e j -> p j e"),
-                        scalar=inv[:, b, h : h + 1],
-                        in1=t_cross[:, b, :, h, :].rearrange("p e j -> p j e"),
-                        op0=ALU.mult,
-                        op1=ALU.add,
-                    )
+                nc.gpsimd.tensor_tensor(
+                    out=result[:, b, :, :, :],
+                    in0=t_same[:, b, :, :, :].rearrange("p h e j -> p h j e"),
+                    in1=t_cross[:, b, :, :, :].rearrange("p h e j -> p h j e"),
+                    op=ALU.add,
+                )
             store(g, m, result)
 
         def copy_out(g, m, acc):
@@ -259,17 +274,39 @@ def tile_attention_pa_kernel(tc, x, freqs_cis, wqkv, q_norm_w, k_norm_w, out_0, 
             )
             store(g, m, result)
 
-        for g in range(N_GROUPS):
+        def prepare_w(g, c):
+            grouped = new_grouped()
+            for b in range(2):
+                transpose_half(grouped, b, w_pieces(g, b, c), False)
+            return grouped
+
+        def quantise_w(g, c, grouped):
+            quantise(grouped, w_operand[g][0][:, c, :], w_operand[g][1][:, c, :])
+
+        load_w(W_BUFS)
+        w_operand[1] = new_w_operand()
+        for i in range(TOKEN_TILES):
+            if i + 1 < TOKEN_TILES:
+                x_grouped = prepare_x(i + 1)
+            acc = multiply(0, i)
+            inv = norms(acc)
+            if i + 1 < TOKEN_TILES:
+                quantise_x(i + 1, x_grouped)
+            else:
+                for c in range(PASSES):
+                    quantise_w(1, c, prepare_w(1, c))
+            rotate(0, i, acc, inv)
+
+        for g in range(1, N_GROUPS):
             if g + W_BUFS < N_GROUPS:
                 load_w(g + W_BUFS)
             if g + 1 < N_GROUPS:
                 w_operand[g + 1] = new_w_operand()
             for i in range(TOKEN_TILES):
                 if g + 1 < N_GROUPS:
-                    grouped = transpose_pass(w_row_tiles(g + 1), i, False)
-                    quantise(grouped, w_operand[g + 1][0], w_operand[g + 1][1], i)
+                    quantise_w(g + 1, i, prepare_w(g + 1, i))
                 acc = multiply(g, i)
                 if g == V_GROUP:
                     copy_out(g, i, acc)
                 else:
-                    norm_and_rotate(g, i, acc)
+                    rotate(g, i, acc, norms(acc))

@@ -22,7 +22,8 @@ PASSES = D // K_PASS
 TOKEN_TILES = TOKENS // P
 HD = 128
 HP = HD // 2
-GROUP = 512
+HEADS = 4
+GROUP = HEADS * HD
 HALF = GROUP // 2
 Q_GROUPS = 4
 K_GROUP = 4
@@ -39,7 +40,7 @@ def tile_attention_pa_kernel(tc, x, freqs_cis, wqkv, q_norm_w, k_norm_w, out_0, 
     with ExitStack() as ctx:
         const = ctx.enter_context(tc.tile_pool(name="const", bufs=1))
         w_pool = ctx.enter_context(tc.tile_pool(name="w_pool", bufs=W_BUFS))
-        stage = ctx.enter_context(tc.tile_pool(name="stage", bufs=6))
+        stage = ctx.enter_context(tc.tile_pool(name="stage", bufs=8))
         quantised = ctx.enter_context(tc.tile_pool(name="quantised", bufs=2))
         work = ctx.enter_context(tc.tile_pool(name="work", bufs=4))
         small = ctx.enter_context(tc.tile_pool(name="small", bufs=4))
@@ -57,10 +58,9 @@ def tile_attention_pa_kernel(tc, x, freqs_cis, wqkv, q_norm_w, k_norm_w, out_0, 
 
         freqs = const.tile([P, 2, HP, 2], BF16, name="freqs")
         nc.scalar.dma_start(out=freqs[:], in_=freqs_cis.rearrange("(a p) j t -> p a j t", p=P))
-        gain_row = const.tile([P, 2, HD], BF16, name="gain_row")
-        nc.vector.memset(gain_row[:], 0.0)
-        nc.scalar.dma_start(out=gain_row[0:1, 0, :], in_=q_norm_w.unsqueeze(0))
-        nc.scalar.dma_start(out=gain_row[0:1, 1, :], in_=k_norm_w.unsqueeze(0))
+        gains = const.tile([P, 2, HP, 2], BF16, name="gains")
+        nc.scalar.dma_start(out=gains[:, 0, :, :].rearrange("p j e -> p (j e)"), in_=q_norm_w.partition_broadcast(P))
+        nc.scalar.dma_start(out=gains[:, 1, :, :].rearrange("p j e -> p (j e)"), in_=k_norm_w.partition_broadcast(P))
 
         x_rows = const.tile([P, TOKEN_TILES, D], BF16, name="x_rows")
 
@@ -70,12 +70,12 @@ def tile_attention_pa_kernel(tc, x, freqs_cis, wqkv, q_norm_w, k_norm_w, out_0, 
         w_rows = {}
 
         def load_w(g):
-            w_rows[g] = w_pool.tile([P, 2, 2, D], BF16, name="w_rows")
+            w_rows[g] = w_pool.tile([P, HEADS, D], BF16, name="w_rows")
             for b in range(2):
                 first = GROUP * g + HALF * b
                 nc.sync.dma_start(
-                    out=w_rows[g][:, b, :, :].rearrange("p e k -> p (e k)"),
-                    in_=wqkv[first : first + HALF, :].rearrange("(p e) k -> p (e k)", e=2),
+                    out=w_rows[g][:, 2 * b : 2 * b + 2, :],
+                    in_=wqkv[first : first + HALF, :].rearrange("(h p) k -> p h k", p=P),
                 )
 
         load_x(0)
@@ -88,16 +88,36 @@ def tile_attention_pa_kernel(tc, x, freqs_cis, wqkv, q_norm_w, k_norm_w, out_0, 
         eps = const.tile([P, 1], F32, name="eps")
         nc.vector.memset(eps[:], EPS)
         warm = const.tile([P, 1], F32, name="warm")
-        nc.scalar.activation(out=warm[:], in_=eps[:], func=ACT.Sqrt)
-        ones = const.tile([P, P], BF16, name="ones")
-        nc.vector.memset(ones[:], 1.0)
+        nc.scalar.activation(out=warm[:], in_=eps[:], func=ACT.Abs_reciprocal_sqrt)
         ident = const.tile([P, P], F32, name="ident")
         make_identity(nc, ident[:])
+        sorter = const.tile([P, 2, HP], F32, name="sorter")
+        nc.vector.tensor_copy(out=sorter[:], in_=ident[:].rearrange("p (j e) -> p e j", e=2))
 
-        def new_grouped():
-            return stage.tile([P, GROUP, PACK], BF16, align_bytes=64, name="grouped")
+        factors = {}
+        for kind in range(2):
+            for a in range(2):
+                table = const.tile([P, 2, 2, HP], F32, name="factors%d%d" % (kind, a))
+                nc.vector.tensor_tensor(
+                    out=table[:, 0, :, :],
+                    in0=gains[:, kind, :, :].rearrange("p j e -> p e j"),
+                    in1=freqs[:, a, :, 0].unsqueeze(1).to_broadcast([P, 2, HP]),
+                    op=ALU.mult,
+                )
+                nc.vector.tensor_tensor(
+                    out=table[:, 1, 0, :], in0=gains[:, kind, :, 0], in1=freqs[:, a, :, 1], op=ALU.mult
+                )
+                nc.vector.scalar_tensor_tensor(
+                    out=table[:, 1, 1, :],
+                    in0=gains[:, kind, :, 1],
+                    scalar=-1.0,
+                    in1=freqs[:, a, :, 1],
+                    op0=ALU.mult,
+                    op1=ALU.mult,
+                )
+                factors[(kind, a)] = table
 
-        def transpose_half(grouped, b, pieces, on_vector):
+        def prepare(pieces, permutation, codes, scales):
             bank = t_psum.tile([P, 2, HALF], F32, name="bank")
             for u in range(2):
                 for i in range(2):
@@ -106,99 +126,48 @@ def tile_attention_pa_kernel(tc, x, freqs_cis, wqkv, q_norm_w, k_norm_w, out_0, 
                     nc.tensor.transpose(
                         out=bank[:, u, P * i : P * (i + 1)],
                         in_=rows.bitcast(F32)[:, first : first + P],
-                        identity=ident[:],
+                        identity=permutation,
                     )
-            dst = grouped[:].bitcast(F32)[:, HALF * b : HALF * (b + 1), :]
-            src = bank[:].rearrange("p u n -> p n u")
-            if on_vector:
-                nc.vector.tensor_copy(out=dst, in_=src)
-            else:
-                nc.scalar.copy(out=dst, in_=src)
-
-        def w_pieces(g, b, c):
-            return [(w_rows[g][:, b, e, :], c) for e in range(2)]
-
-        def x_pieces(m, b):
-            return [(x_rows[:, m, :], 2 * b + i) for i in range(2)]
-
-        def quantise(grouped, codes, scales):
+            grouped = stage.tile([P, HALF, PACK], BF16, align_bytes=64, name="grouped")
+            nc.scalar.copy(out=grouped[:].bitcast(F32), in_=bank[:].rearrange("p u n -> p n u"))
             nc.vector.quantize_mx(
                 out=codes.bitcast(FP8X4), scales=scales, in_=grouped[:].rearrange("p n t -> p (n t)")
             )
-
-        def new_w_operand():
-            codes = quantised.tile([P, PASSES, GROUP], U32, align_bytes=64, name="w_codes")
-            scales = quantised.tile([P, PASSES, GROUP], U8, align_bytes=64, name="w_scales")
-            return codes, scales
 
         x_codes = const.tile([P, TOKEN_TILES, PASSES * P], U32, align_bytes=64, name="x_codes")
         x_scales = const.tile([P, TOKEN_TILES, PASSES * P], U8, align_bytes=64, name="x_scales")
 
         def prepare_x(m):
-            grouped = new_grouped()
             for b in range(2):
-                transpose_half(grouped, b, x_pieces(m, b), b == 1)
-            return grouped
-
-        def quantise_x(m, grouped):
-            quantise(grouped, x_codes[:, m, :], x_scales[:, m, :])
-
-        w_operand = {0: new_w_operand()}
-        x_grouped = prepare_x(0)
-        first_grouped = [new_grouped() for c in range(PASSES)]
-        for c in range(PASSES):
-            transpose_half(first_grouped[c], 0, w_pieces(0, 0, c), c % 2 == 1)
-        quantise_x(0, x_grouped)
-
-        gain_bank = t_psum.tile([P, 2, HALF], F32, name="bank")
-        nc.tensor.matmul(
-            out=gain_bank[:, 0, :],
-            lhsT=ones[:],
-            rhs=gain_row[:].rearrange("p a d -> p (a d)"),
-            start=True,
-            stop=True,
-        )
-        gains = const.tile([P, 2, HP, 2], F32, name="gains")
-        nc.scalar.copy(out=gains[:].rearrange("p a j e -> p (a j e)"), in_=gain_bank[:, 0, :])
-
-        same = {}
-        cross = {}
-        for kind in range(2):
-            for a in range(2):
-                same_t = const.tile([P, 2, HP], F32, name="same%d%d" % (kind, a))
-                cross_t = const.tile([P, 2, HP], F32, name="cross%d%d" % (kind, a))
-                nc.vector.tensor_tensor(
-                    out=same_t[:],
-                    in0=gains[:, kind, :, :].rearrange("p j e -> p e j"),
-                    in1=freqs[:, a, :, 0].unsqueeze(1).to_broadcast([P, 2, HP]),
-                    op=ALU.mult,
+                prepare(
+                    [(x_rows[:, m, :], 2 * b + i) for i in range(2)],
+                    ident[:],
+                    x_codes[:, m, HALF * b : HALF * (b + 1)],
+                    x_scales[:, m, HALF * b : HALF * (b + 1)],
                 )
-                nc.vector.scalar_tensor_tensor(
-                    out=cross_t[:, 0, :],
-                    in0=gains[:, kind, :, 1],
-                    scalar=-1.0,
-                    in1=freqs[:, a, :, 1],
-                    op0=ALU.mult,
-                    op1=ALU.mult,
-                )
-                nc.vector.tensor_tensor(
-                    out=cross_t[:, 1, :], in0=gains[:, kind, :, 0], in1=freqs[:, a, :, 1], op=ALU.mult
-                )
-                same[(kind, a)] = same_t
-                cross[(kind, a)] = cross_t
 
-        for c in range(PASSES):
-            transpose_half(first_grouped[c], 1, w_pieces(0, 1, c), c % 2 == 1)
-            if c >= 1:
-                quantise(first_grouped[c - 1], w_operand[0][0][:, c - 1, :], w_operand[0][1][:, c - 1, :])
-        quantise(first_grouped[PASSES - 1], w_operand[0][0][:, PASSES - 1, :], w_operand[0][1][:, PASSES - 1, :])
+        w_operand = {}
 
-        def multiply(g, m):
-            acc = acc_psum.tile([P, 2, 2, 2, HP], F32, name="acc")
+        def new_w_operand(g):
+            codes = quantised.tile([P, PASSES, GROUP], U32, align_bytes=64, name="w_codes")
+            scales = quantised.tile([P, PASSES, GROUP], U8, align_bytes=64, name="w_scales")
+            w_operand[g] = (codes, scales)
+
+        def prepare_w(g, c, b):
+            permutation = ident[:] if g == V_GROUP else sorter[:].rearrange("p e j -> p (e j)")
+            codes, scales = w_operand[g]
+            prepare(
+                [(w_rows[g][:, 2 * b + i, :], c) for i in range(2)],
+                permutation,
+                codes[:, c, HALF * b : HALF * (b + 1)],
+                scales[:, c, HALF * b : HALF * (b + 1)],
+            )
+
+        def multiply(g, m, acc):
             codes, scales = w_operand[g]
             for c in range(PASSES):
                 nc.tensor.matmul_mx(
-                    out=acc[:].rearrange("p b e h j -> p (b e h j)"),
+                    out=acc,
                     lhsT=x_codes[:, m, P * c : P * (c + 1)].bitcast(FP8X4),
                     lhsT_scale=x_scales[:, m, P * c : P * (c + 1)],
                     rhs=codes[:, c, :].bitcast(FP8X4),
@@ -206,7 +175,6 @@ def tile_attention_pa_kernel(tc, x, freqs_cis, wqkv, q_norm_w, k_norm_w, out_0, 
                     start=(c == 0),
                     stop=(c == PASSES - 1),
                 )
-            return acc
 
         def store(g, m, result):
             if g < Q_GROUPS:
@@ -215,98 +183,84 @@ def tile_attention_pa_kernel(tc, x, freqs_cis, wqkv, q_norm_w, k_norm_w, out_0, 
                 dst = out_dram[1][P * m : P * (m + 1), :]
             else:
                 dst = out_dram[2][P * m : P * (m + 1), :]
-            nc.sync.dma_start(out=dst, in_=result[:].rearrange("p b h j e -> p (b h j e)"))
+            nc.sync.dma_start(out=dst, in_=result)
 
-        def norms(acc):
-            sumsq = small.tile([P, 2, 2], F32, name="sumsq")
-            for b in range(2):
-                for h in range(2):
-                    squares = small.tile([P, 2, HP], BF16, name="squares")
-                    nc.scalar.activation(
-                        out=squares[:], in_=acc[:, b, :, h, :], func=ACT.Square, accum_out=sumsq[:, b, h : h + 1]
-                    )
-            rms = small.tile([P, 2, 2], F32, name="rms")
-            nc.scalar.activation(out=rms[:], in_=sumsq[:], func=ACT.Sqrt, bias=eps[:, 0:1], scale=1.0 / HD)
-            inv = small.tile([P, 2, 2], F32, name="inv")
-            nc.vector.reciprocal(out=inv[:], in_=rms[:])
-            return inv
+        def product_and_norms(g, m):
+            acc = acc_psum.tile([P, HEADS, 2, HP], F32, name="acc")
+            multiply(g, m, acc[:].rearrange("p h e j -> p (h e j)"))
+            sumsq = small.tile([P, HEADS], F32, name="sumsq")
+            for h in range(HEADS):
+                squares = small.tile([P, HD], BF16, name="squares")
+                nc.scalar.activation(
+                    out=squares[:],
+                    in_=acc[:, h, :, :].rearrange("p e j -> p (e j)"),
+                    func=ACT.Square,
+                    accum_out=sumsq[:, h : h + 1],
+                )
+            inv = small.tile([P, HEADS], F32, name="inv")
+            nc.scalar.activation(
+                out=inv[:], in_=sumsq[:], func=ACT.Abs_reciprocal_sqrt, bias=eps[:, 0:1], scale=1.0 / HD
+            )
+            return acc, inv
 
         def rotate(g, m, acc, inv):
             kind = 0 if g < Q_GROUPS else 1
-            same_t = same[(kind, m % 2)]
-            cross_t = cross[(kind, m % 2)]
-            t_same = work.tile([P, 2, 2, 2, HP], F32, name="t_same")
-            t_cross = work.tile([P, 2, 2, 2, HP], F32, name="t_cross")
-            for b in range(2):
-                for h in range(2):
-                    nc.vector.scalar_tensor_tensor(
-                        out=t_same[:, b, h, :, :],
-                        in0=acc[:, b, :, h, :],
-                        scalar=inv[:, b, h : h + 1],
-                        in1=same_t[:],
-                        op0=ALU.mult,
-                        op1=ALU.mult,
-                    )
-                    for e in range(2):
-                        nc.vector.scalar_tensor_tensor(
-                            out=t_cross[:, b, h, e, :],
-                            in0=acc[:, b, 1 - e, h, :],
-                            scalar=inv[:, b, h : h + 1],
-                            in1=cross_t[:, e, :],
-                            op0=ALU.mult,
-                            op1=ALU.mult,
-                        )
-            result = work.tile([P, 2, 2, HP, 2], F32, name="result")
-            for b in range(2):
-                nc.gpsimd.tensor_tensor(
-                    out=result[:, b, :, :, :],
-                    in0=t_same[:, b, :, :, :].rearrange("p h e j -> p h j e"),
-                    in1=t_cross[:, b, :, :, :].rearrange("p h e j -> p h j e"),
-                    op=ALU.add,
+            table = factors[(kind, m % 2)]
+            products = work.tile([P, 2, HEADS, 2, HP], F32, name="products")
+            for h in range(HEADS):
+                nc.vector.scalar_tensor_tensor(
+                    out=products[:, :, h, :, :].rearrange("p k e j -> p k (e j)"),
+                    in0=acc[:, h, :, :].rearrange("p e j -> p (e j)").unsqueeze(1).to_broadcast([P, 2, HD]),
+                    scalar=inv[:, h : h + 1],
+                    in1=table[:].rearrange("p k e j -> p k (e j)"),
+                    op0=ALU.mult,
+                    op1=ALU.mult,
                 )
-            store(g, m, result)
-
-        def copy_out(g, m, acc):
-            result = work.tile([P, 2, 2, HP, 2], F32, name="result")
-            nc.scalar.copy(
-                out=result[:].rearrange("p b h j e -> p b (h j) e"),
-                in_=acc[:].rearrange("p b e h j -> p b (h j) e"),
+            result = work.tile([P, HEADS, HP, 2], F32, name="result")
+            nc.vector.tensor_tensor(
+                out=result[:],
+                in0=products[:, 0, :, :, :].rearrange("p h e j -> p h j e"),
+                in1=products[:, 1, :, ::-1, :].rearrange("p h e j -> p h j e"),
+                op=ALU.add,
             )
-            store(g, m, result)
+            store(g, m, result[:].rearrange("p h j e -> p (h j e)"))
 
-        def prepare_w(g, c):
-            grouped = new_grouped()
-            for b in range(2):
-                transpose_half(grouped, b, w_pieces(g, b, c), False)
-            return grouped
+        def product_of_v(m):
+            acc = t_psum.tile([P, 2, HALF], F32, name="bank")
+            multiply(V_GROUP, m, acc[:].rearrange("p u n -> p (u n)"))
+            v_result = work.tile([P, GROUP], F32, name="v_result")
+            nc.scalar.copy(out=v_result[:], in_=acc[:].rearrange("p u n -> p (u n)"))
+            store(V_GROUP, m, v_result[:])
 
-        def quantise_w(g, c, grouped):
-            quantise(grouped, w_operand[g][0][:, c, :], w_operand[g][1][:, c, :])
+        new_w_operand(0)
+        prepare_x(0)
+        for b in range(2):
+            for c in range(PASSES):
+                prepare_w(0, c, b)
+        for m in range(1, TOKEN_TILES):
+            prepare_x(m)
 
         load_w(W_BUFS)
-        w_operand[1] = new_w_operand()
-        for i in range(TOKEN_TILES):
-            if i + 1 < TOKEN_TILES:
-                x_grouped = prepare_x(i + 1)
-            acc = multiply(0, i)
-            inv = norms(acc)
-            if i + 1 < TOKEN_TILES:
-                quantise_x(i + 1, x_grouped)
-            else:
+        new_w_operand(1)
+        for m in range(TOKEN_TILES):
+            acc, inv = product_and_norms(0, m)
+            if m == TOKEN_TILES - 1:
                 for c in range(PASSES):
-                    quantise_w(1, c, prepare_w(1, c))
-            rotate(0, i, acc, inv)
+                    for b in range(2):
+                        prepare_w(1, c, b)
+            rotate(0, m, acc, inv)
 
-        for g in range(1, N_GROUPS):
+        for g in range(1, V_GROUP):
             if g + W_BUFS < N_GROUPS:
                 load_w(g + W_BUFS)
-            if g + 1 < N_GROUPS:
-                w_operand[g + 1] = new_w_operand()
-            for i in range(TOKEN_TILES):
-                if g + 1 < N_GROUPS:
-                    quantise_w(g + 1, i, prepare_w(g + 1, i))
-                acc = multiply(g, i)
-                if g == V_GROUP:
-                    copy_out(g, i, acc)
-                else:
-                    rotate(g, i, acc, norms(acc))
+            new_w_operand(g + 1)
+            for m in range(TOKEN_TILES):
+                if m < 2:
+                    for c in range(2 * m, 2 * m + 2):
+                        for b in range(2):
+                            prepare_w(g + 1, c, b)
+                acc, inv = product_and_norms(g, m)
+                rotate(g, m, acc, inv)
+                if g == K_GROUP and m >= 2:
+                    for v_tile in range(2 * (m - 2), 2 * (m - 2) + 2):
+                        product_of_v(v_tile)

@@ -56,11 +56,9 @@ def tile_attention_pa_kernel(tc, x, freqs_cis, wqkv, q_norm_w, k_norm_w, out_0, 
             out_2.rearrange("b s h d -> (b s) (h d)"),
         ]
 
+        gain_row = const.tile([P, 2, HD], BF16, name="gain_row")
+        nc.vector.memset(gain_row[:], 0.0)
         freqs = const.tile([P, 2, HP, 2], BF16, name="freqs")
-        nc.scalar.dma_start(out=freqs[:], in_=freqs_cis.rearrange("(a p) j t -> p a j t", p=P))
-        gains = const.tile([P, 2, HP, 2], BF16, name="gains")
-        nc.scalar.dma_start(out=gains[:, 0, :, :].rearrange("p j e -> p (j e)"), in_=q_norm_w.partition_broadcast(P))
-        nc.scalar.dma_start(out=gains[:, 1, :, :].rearrange("p j e -> p (j e)"), in_=k_norm_w.partition_broadcast(P))
 
         x_rows = const.tile([P, TOKEN_TILES, D], BF16, name="x_rows")
 
@@ -80,6 +78,9 @@ def tile_attention_pa_kernel(tc, x, freqs_cis, wqkv, q_norm_w, k_norm_w, out_0, 
 
         load_x(0)
         load_w(0)
+        nc.sync.dma_start(out=gain_row[0:1, 0, :], in_=q_norm_w.unsqueeze(0))
+        nc.sync.dma_start(out=gain_row[0:1, 1, :], in_=k_norm_w.unsqueeze(0))
+        nc.sync.dma_start(out=freqs[:], in_=freqs_cis.rearrange("(a p) j t -> p a j t", p=P))
         for m in range(1, TOKEN_TILES):
             load_x(m)
         for g in range(1, W_BUFS):
@@ -89,33 +90,48 @@ def tile_attention_pa_kernel(tc, x, freqs_cis, wqkv, q_norm_w, k_norm_w, out_0, 
         nc.vector.memset(eps[:], EPS)
         warm = const.tile([P, 1], F32, name="warm")
         nc.scalar.activation(out=warm[:], in_=eps[:], func=ACT.Abs_reciprocal_sqrt)
+        ones = const.tile([P, P], BF16, name="ones")
+        nc.vector.memset(ones[:], 1.0)
         ident = const.tile([P, P], F32, name="ident")
         make_identity(nc, ident[:])
         sorter = const.tile([P, 2, HP], F32, name="sorter")
         nc.vector.tensor_copy(out=sorter[:], in_=ident[:].rearrange("p (j e) -> p e j", e=2))
 
+        gains = const.tile([P, 2, HP, 2], F32, name="gains")
+
+        def spread_gains():
+            gain_bank = t_psum.tile([P, 2, HALF], F32, name="bank")
+            nc.tensor.matmul(
+                out=gain_bank[:, 0, :],
+                lhsT=ones[:],
+                rhs=gain_row[:].rearrange("p a d -> p (a d)"),
+                start=True,
+                stop=True,
+            )
+            nc.scalar.copy(out=gains[:].rearrange("p a j e -> p (a j e)"), in_=gain_bank[:, 0, :])
+
         factors = {}
-        for kind in range(2):
-            for a in range(2):
-                table = const.tile([P, 2, 2, HP], F32, name="factors%d%d" % (kind, a))
-                nc.vector.tensor_tensor(
-                    out=table[:, 0, :, :],
-                    in0=gains[:, kind, :, :].rearrange("p j e -> p e j"),
-                    in1=freqs[:, a, :, 0].unsqueeze(1).to_broadcast([P, 2, HP]),
-                    op=ALU.mult,
-                )
-                nc.vector.tensor_tensor(
-                    out=table[:, 1, 0, :], in0=gains[:, kind, :, 0], in1=freqs[:, a, :, 1], op=ALU.mult
-                )
-                nc.vector.scalar_tensor_tensor(
-                    out=table[:, 1, 1, :],
-                    in0=gains[:, kind, :, 1],
-                    scalar=-1.0,
-                    in1=freqs[:, a, :, 1],
-                    op0=ALU.mult,
-                    op1=ALU.mult,
-                )
-                factors[(kind, a)] = table
+
+        def make_factors(kind, a):
+            table = const.tile([P, 2, 2, HP], F32, name="factors%d%d" % (kind, a))
+            nc.vector.tensor_tensor(
+                out=table[:, 0, :, :],
+                in0=gains[:, kind, :, :].rearrange("p j e -> p e j"),
+                in1=freqs[:, a, :, 0].unsqueeze(1).to_broadcast([P, 2, HP]),
+                op=ALU.mult,
+            )
+            nc.vector.tensor_tensor(
+                out=table[:, 1, 0, :], in0=gains[:, kind, :, 0], in1=freqs[:, a, :, 1], op=ALU.mult
+            )
+            nc.vector.scalar_tensor_tensor(
+                out=table[:, 1, 1, :],
+                in0=gains[:, kind, :, 1],
+                scalar=-1.0,
+                in1=freqs[:, a, :, 1],
+                op0=ALU.mult,
+                op1=ALU.mult,
+            )
+            factors[(kind, a)] = table
 
         def prepare(pieces, permutation, codes, scales):
             bank = t_psum.tile([P, 2, HALF], F32, name="bank")
@@ -203,7 +219,7 @@ def tile_attention_pa_kernel(tc, x, freqs_cis, wqkv, q_norm_w, k_norm_w, out_0, 
             )
             return acc, inv
 
-        def rotate(g, m, acc, inv):
+        def multiply_by_factors(g, m, acc, inv):
             kind = 0 if g < Q_GROUPS else 1
             table = factors[(kind, m % 2)]
             products = work.tile([P, 2, HEADS, 2, HP], F32, name="products")
@@ -216,6 +232,9 @@ def tile_attention_pa_kernel(tc, x, freqs_cis, wqkv, q_norm_w, k_norm_w, out_0, 
                     op0=ALU.mult,
                     op1=ALU.mult,
                 )
+            return g, m, products
+
+        def add_and_store(g, m, products):
             result = work.tile([P, HEADS, HP, 2], F32, name="result")
             nc.vector.tensor_tensor(
                 out=result[:],
@@ -237,18 +256,25 @@ def tile_attention_pa_kernel(tc, x, freqs_cis, wqkv, q_norm_w, k_norm_w, out_0, 
         for b in range(2):
             for c in range(PASSES):
                 prepare_w(0, c, b)
+        spread_gains()
         for m in range(1, TOKEN_TILES):
             prepare_x(m)
+        for kind in range(2):
+            for a in range(2):
+                make_factors(kind, a)
 
         load_w(W_BUFS)
         new_w_operand(1)
+        waiting = []
         for m in range(TOKEN_TILES):
             acc, inv = product_and_norms(0, m)
             if m == TOKEN_TILES - 1:
                 for c in range(PASSES):
                     for b in range(2):
                         prepare_w(1, c, b)
-            rotate(0, m, acc, inv)
+            waiting.append(multiply_by_factors(0, m, acc, inv))
+            if len(waiting) > 1:
+                add_and_store(*waiting[-2])
 
         for g in range(1, V_GROUP):
             if g + W_BUFS < N_GROUPS:
@@ -260,7 +286,9 @@ def tile_attention_pa_kernel(tc, x, freqs_cis, wqkv, q_norm_w, k_norm_w, out_0, 
                         for b in range(2):
                             prepare_w(g + 1, c, b)
                 acc, inv = product_and_norms(g, m)
-                rotate(g, m, acc, inv)
+                waiting.append(multiply_by_factors(g, m, acc, inv))
+                add_and_store(*waiting[-2])
                 if g == K_GROUP and m >= 2:
                     for v_tile in range(2 * (m - 2), 2 * (m - 2) + 2):
                         product_of_v(v_tile)
+        add_and_store(*waiting[-1])

@@ -40,7 +40,7 @@ def tile_attention_pa_kernel(tc, x, freqs_cis, wqkv, q_norm_w, k_norm_w, out_0, 
     with ExitStack() as ctx:
         const = ctx.enter_context(tc.tile_pool(name="const", bufs=1))
         w_pool = ctx.enter_context(tc.tile_pool(name="w_pool", bufs=W_BUFS))
-        stage = ctx.enter_context(tc.tile_pool(name="stage", bufs=8))
+        stage = ctx.enter_context(tc.tile_pool(name="stage", bufs=4))
         quantised = ctx.enter_context(tc.tile_pool(name="quantised", bufs=2))
         work = ctx.enter_context(tc.tile_pool(name="work", bufs=4))
         small = ctx.enter_context(tc.tile_pool(name="small", bufs=4))
@@ -134,18 +134,23 @@ def tile_attention_pa_kernel(tc, x, freqs_cis, wqkv, q_norm_w, k_norm_w, out_0, 
             factors[(kind, a)] = table
 
         def prepare(pieces, permutation, codes, scales):
-            bank = t_psum.tile([P, 2, HALF], F32, name="bank")
-            for u in range(2):
-                for i in range(2):
-                    rows, c = pieces[i]
-                    first = WORDS_PASS * c + P * u
-                    nc.tensor.transpose(
-                        out=bank[:, u, P * i : P * (i + 1)],
-                        in_=rows.bitcast(F32)[:, first : first + P],
-                        identity=permutation,
-                    )
-            grouped = stage.tile([P, HALF, PACK], BF16, align_bytes=64, name="grouped")
-            nc.scalar.copy(out=grouped[:].bitcast(F32), in_=bank[:].rearrange("p u n -> p n u"))
+            banks = len(pieces) // 2
+            grouped = stage.tile([P, banks * HALF, PACK], BF16, align_bytes=64, name="grouped%d" % banks)
+            for n in range(banks):
+                bank = t_psum.tile([P, 2, HALF], F32, name="bank")
+                for u in range(2):
+                    for i in range(2):
+                        rows, c = pieces[2 * n + i]
+                        first = WORDS_PASS * c + P * u
+                        nc.tensor.transpose(
+                            out=bank[:, u, P * i : P * (i + 1)],
+                            in_=rows.bitcast(F32)[:, first : first + P],
+                            identity=permutation,
+                        )
+                nc.scalar.copy(
+                    out=grouped[:].bitcast(F32)[:, HALF * n : HALF * (n + 1), :],
+                    in_=bank[:].rearrange("p u n -> p n u"),
+                )
             nc.vector.quantize_mx(
                 out=codes.bitcast(FP8X4), scales=scales, in_=grouped[:].rearrange("p n t -> p (n t)")
             )
@@ -154,13 +159,7 @@ def tile_attention_pa_kernel(tc, x, freqs_cis, wqkv, q_norm_w, k_norm_w, out_0, 
         x_scales = const.tile([P, TOKEN_TILES, PASSES * P], U8, align_bytes=64, name="x_scales")
 
         def prepare_x(m):
-            for b in range(2):
-                prepare(
-                    [(x_rows[:, m, :], 2 * b + i) for i in range(2)],
-                    ident[:],
-                    x_codes[:, m, HALF * b : HALF * (b + 1)],
-                    x_scales[:, m, HALF * b : HALF * (b + 1)],
-                )
+            prepare([(x_rows[:, m, :], c) for c in range(PASSES)], ident[:], x_codes[:, m, :], x_scales[:, m, :])
 
         w_operand = {}
 
@@ -169,14 +168,25 @@ def tile_attention_pa_kernel(tc, x, freqs_cis, wqkv, q_norm_w, k_norm_w, out_0, 
             scales = quantised.tile([P, PASSES, GROUP], U8, align_bytes=64, name="w_scales")
             w_operand[g] = (codes, scales)
 
-        def prepare_w(g, c, b):
-            permutation = ident[:] if g == V_GROUP else sorter[:].rearrange("p e j -> p (e j)")
+        def w_permutation(g):
+            return ident[:] if g == V_GROUP else sorter[:].rearrange("p e j -> p (e j)")
+
+        def prepare_half_pass(g, c, b):
             codes, scales = w_operand[g]
             prepare(
                 [(w_rows[g][:, 2 * b + i, :], c) for i in range(2)],
-                permutation,
+                w_permutation(g),
                 codes[:, c, HALF * b : HALF * (b + 1)],
                 scales[:, c, HALF * b : HALF * (b + 1)],
+            )
+
+        def prepare_two_passes(g, c):
+            codes, scales = w_operand[g]
+            prepare(
+                [(w_rows[g][:, h, :], c + i) for i in range(2) for h in range(HEADS)],
+                w_permutation(g),
+                codes[:, c : c + 2, :].rearrange("p c n -> p (c n)"),
+                scales[:, c : c + 2, :].rearrange("p c n -> p (c n)"),
             )
 
         def multiply(g, m, acc):
@@ -255,7 +265,7 @@ def tile_attention_pa_kernel(tc, x, freqs_cis, wqkv, q_norm_w, k_norm_w, out_0, 
         prepare_x(0)
         for b in range(2):
             for c in range(PASSES):
-                prepare_w(0, c, b)
+                prepare_half_pass(0, c, b)
         spread_gains()
         for m in range(1, TOKEN_TILES):
             prepare_x(m)
@@ -269,9 +279,8 @@ def tile_attention_pa_kernel(tc, x, freqs_cis, wqkv, q_norm_w, k_norm_w, out_0, 
         for m in range(TOKEN_TILES):
             acc, inv = product_and_norms(0, m)
             if m == TOKEN_TILES - 1:
-                for c in range(PASSES):
-                    for b in range(2):
-                        prepare_w(1, c, b)
+                for c in range(0, PASSES, 2):
+                    prepare_two_passes(1, c)
             waiting.append(multiply_by_factors(0, m, acc, inv))
             if len(waiting) > 1:
                 add_and_store(*waiting[-2])
@@ -282,9 +291,7 @@ def tile_attention_pa_kernel(tc, x, freqs_cis, wqkv, q_norm_w, k_norm_w, out_0, 
             new_w_operand(g + 1)
             for m in range(TOKEN_TILES):
                 if m < 2:
-                    for c in range(2 * m, 2 * m + 2):
-                        for b in range(2):
-                            prepare_w(g + 1, c, b)
+                    prepare_two_passes(g + 1, 2 * m)
                 acc, inv = product_and_norms(g, m)
                 waiting.append(multiply_by_factors(g, m, acc, inv))
                 add_and_store(*waiting[-2])

@@ -246,7 +246,7 @@ def tile_attention_pa_kernel(tc, x, freqs_cis, wqkv, q_norm_w, k_norm_w, out_0, 
 
         def add_and_store(g, m, products):
             result = work.tile([P, HEADS, HP, 2], F32, name="result")
-            nc.vector.tensor_tensor(
+            nc.gpsimd.tensor_tensor(
                 out=result[:],
                 in0=products[:, 0, :, :, :].rearrange("p h e j -> p h j e"),
                 in1=products[:, 1, :, ::-1, :].rearrange("p h e j -> p h j e"),

@@ -94,8 +94,6 @@ def tile_attention_pa_kernel(tc, x, freqs_cis, wqkv, q_norm_w, k_norm_w, out_0, 
         nc.vector.memset(ones[:], 1.0)
         ident = const.tile([P, P], F32, name="ident")
         make_identity(nc, ident[:])
-        sorter = const.tile([P, 2, HP], F32, name="sorter")
-        nc.vector.tensor_copy(out=sorter[:], in_=ident[:].rearrange("p (j e) -> p e j", e=2))
 
         gains = const.tile([P, 2, HP, 2], F32, name="gains")
 
@@ -113,18 +111,18 @@ def tile_attention_pa_kernel(tc, x, freqs_cis, wqkv, q_norm_w, k_norm_w, out_0, 
         factors = {}
 
         def make_factors(kind, a):
-            table = const.tile([P, 2, 2, HP], F32, name="factors%d%d" % (kind, a))
+            table = const.tile([P, 2, HP, 2], F32, name="factors%d%d" % (kind, a))
             nc.vector.tensor_tensor(
                 out=table[:, 0, :, :],
-                in0=gains[:, kind, :, :].rearrange("p j e -> p e j"),
-                in1=freqs[:, a, :, 0].unsqueeze(1).to_broadcast([P, 2, HP]),
+                in0=gains[:, kind, :, :],
+                in1=freqs[:, a, :, 0].unsqueeze(2).to_broadcast([P, HP, 2]),
                 op=ALU.mult,
             )
             nc.vector.tensor_tensor(
-                out=table[:, 1, 0, :], in0=gains[:, kind, :, 0], in1=freqs[:, a, :, 1], op=ALU.mult
+                out=table[:, 1, :, 0], in0=gains[:, kind, :, 0], in1=freqs[:, a, :, 1], op=ALU.mult
             )
             nc.vector.scalar_tensor_tensor(
-                out=table[:, 1, 1, :],
+                out=table[:, 1, :, 1],
                 in0=gains[:, kind, :, 1],
                 scalar=-1.0,
                 in1=freqs[:, a, :, 1],
@@ -169,7 +167,7 @@ def tile_attention_pa_kernel(tc, x, freqs_cis, wqkv, q_norm_w, k_norm_w, out_0, 
             w_operand[g] = (codes, scales)
 
         def w_permutation(g):
-            return ident[:] if g == V_GROUP else sorter[:].rearrange("p e j -> p (e j)")
+            return ident[:]
 
         def prepare_half_pass(g, c, b):
             codes, scales = w_operand[g]
@@ -212,14 +210,14 @@ def tile_attention_pa_kernel(tc, x, freqs_cis, wqkv, q_norm_w, k_norm_w, out_0, 
             nc.sync.dma_start(out=dst, in_=result)
 
         def product_and_norms(g, m):
-            acc = acc_psum.tile([P, HEADS, 2, HP], F32, name="acc")
-            multiply(g, m, acc[:].rearrange("p h e j -> p (h e j)"))
+            acc = acc_psum.tile([P, HEADS, HD], F32, name="acc")
+            multiply(g, m, acc[:].rearrange("p h d -> p (h d)"))
             sumsq = small.tile([P, HEADS], F32, name="sumsq")
             for h in range(HEADS):
                 squares = small.tile([P, HD], BF16, name="squares")
                 nc.scalar.activation(
                     out=squares[:],
-                    in_=acc[:, h, :, :].rearrange("p e j -> p (e j)"),
+                    in_=acc[:, h, :],
                     func=ACT.Square,
                     accum_out=sumsq[:, h : h + 1],
                 )
@@ -232,27 +230,24 @@ def tile_attention_pa_kernel(tc, x, freqs_cis, wqkv, q_norm_w, k_norm_w, out_0, 
         def multiply_by_factors(g, m, acc, inv):
             kind = 0 if g < Q_GROUPS else 1
             table = factors[(kind, m % 2)]
-            products = work.tile([P, 2, HEADS, 2, HP], F32, name="products")
+            products = work.tile([P, 2, HEADS * HP, 2], F32, name="products")
             for h in range(HEADS):
                 nc.vector.scalar_tensor_tensor(
-                    out=products[:, :, h, :, :].rearrange("p k e j -> p k (e j)"),
-                    in0=acc[:, h, :, :].rearrange("p e j -> p (e j)").unsqueeze(1).to_broadcast([P, 2, HD]),
+                    out=products[:, :, HP * h : HP * (h + 1), :].rearrange("p k j e -> p k (j e)"),
+                    in0=acc[:, h, :].unsqueeze(1).to_broadcast([P, 2, HD]),
                     scalar=inv[:, h : h + 1],
-                    in1=table[:].rearrange("p k e j -> p k (e j)"),
+                    in1=table[:].rearrange("p k j e -> p k (j e)"),
                     op0=ALU.mult,
                     op1=ALU.mult,
                 )
             return g, m, products
 
         def add_and_store(g, m, products):
-            result = work.tile([P, HEADS, HP, 2], F32, name="result")
+            result = work.tile([P, HEADS * HP, 2], F32, name="result")
             nc.gpsimd.tensor_tensor(
-                out=result[:],
-                in0=products[:, 0, :, :, :].rearrange("p h e j -> p h j e"),
-                in1=products[:, 1, :, ::-1, :].rearrange("p h e j -> p h j e"),
-                op=ALU.add,
+                out=result[:], in0=products[:, 0, :, :], in1=products[:, 1, :, ::-1], op=ALU.add
             )
-            store(g, m, result[:].rearrange("p h j e -> p (h j e)"))
+            store(g, m, result[:].rearrange("p n e -> p (n e)"))
 
         def product_of_v(m):
             acc = t_psum.tile([P, 2, HALF], F32, name="bank")

@@ -131,7 +131,7 @@ def tile_attention_pa_kernel(tc, x, freqs_cis, wqkv, q_norm_w, k_norm_w, out_0, 
             )
             factors[(kind, a)] = table
 
-        def prepare(pieces, permutation, codes, scales):
+        def prepare(pieces, permutation, codes, scales, hold_gpsimd=False):
             banks = len(pieces) // 2
             grouped = stage.tile([P, banks * HALF, PACK], BF16, align_bytes=64, name="grouped%d" % banks)
             for n in range(banks):
@@ -152,6 +152,9 @@ def tile_attention_pa_kernel(tc, x, freqs_cis, wqkv, q_norm_w, k_norm_w, out_0, 
             nc.vector.quantize_mx(
                 out=codes.bitcast(FP8X4), scales=scales, in_=grouped[:].rearrange("p n t -> p (n t)")
             )
+            if hold_gpsimd:
+                held = small.tile([P, 1], U32, name="held")
+                nc.gpsimd.tensor_copy(out=held[:], in_=codes[:, 0:1])
 
         x_codes = const.tile([P, TOKEN_TILES, PASSES * P], U32, align_bytes=64, name="x_codes")
         x_scales = const.tile([P, TOKEN_TILES, PASSES * P], U8, align_bytes=64, name="x_scales")
@@ -185,6 +188,7 @@ def tile_attention_pa_kernel(tc, x, freqs_cis, wqkv, q_norm_w, k_norm_w, out_0, 
                 w_permutation(g),
                 codes[:, c : c + 2, :].rearrange("p c n -> p (c n)"),
                 scales[:, c : c + 2, :].rearrange("p c n -> p (c n)"),
+                hold_gpsimd=True,
             )
 
         def multiply(g, m, acc):

@@ -131,7 +131,7 @@ def tile_attention_pa_kernel(tc, x, freqs_cis, wqkv, q_norm_w, k_norm_w, out_0, 
             )
             factors[(kind, a)] = table
 
-        def prepare(pieces, permutation, codes, scales, hold_gpsimd=False):
+        def transpose_and_copy(pieces, permutation):
             banks = len(pieces) // 2
             grouped = stage.tile([P, banks * HALF, PACK], BF16, align_bytes=64, name="grouped%d" % banks)
             for n in range(banks):
@@ -149,12 +149,19 @@ def tile_attention_pa_kernel(tc, x, freqs_cis, wqkv, q_norm_w, k_norm_w, out_0, 
                     out=grouped[:].bitcast(F32)[:, HALF * n : HALF * (n + 1), :],
                     in_=bank[:].rearrange("p u n -> p n u"),
                 )
+            return grouped
+
+        def quantise(grouped, codes, scales):
             nc.vector.quantize_mx(
                 out=codes.bitcast(FP8X4), scales=scales, in_=grouped[:].rearrange("p n t -> p (n t)")
             )
-            if hold_gpsimd:
-                held = small.tile([P, 1], U32, name="held")
-                nc.gpsimd.tensor_copy(out=held[:], in_=codes[:, 0:1])
+
+        def prepare(pieces, permutation, codes, scales):
+            quantise(transpose_and_copy(pieces, permutation), codes, scales)
+
+        def hold_gpsimd(codes):
+            held = small.tile([P, 1], U32, name="held")
+            nc.gpsimd.tensor_copy(out=held[:], in_=codes[:, 0:1])
 
         x_codes = const.tile([P, TOKEN_TILES, PASSES * P], U32, align_bytes=64, name="x_codes")
         x_scales = const.tile([P, TOKEN_TILES, PASSES * P], U8, align_bytes=64, name="x_scales")
@@ -181,15 +188,22 @@ def tile_attention_pa_kernel(tc, x, freqs_cis, wqkv, q_norm_w, k_norm_w, out_0, 
                 scales[:, c, HALF * b : HALF * (b + 1)],
             )
 
-        def prepare_two_passes(g, c):
-            codes, scales = w_operand[g]
-            prepare(
-                [(w_rows[g][:, h, :], c + i) for i in range(2) for h in range(HEADS)],
-                w_permutation(g),
-                codes[:, c : c + 2, :].rearrange("p c n -> p (c n)"),
-                scales[:, c : c + 2, :].rearrange("p c n -> p (c n)"),
-                hold_gpsimd=True,
+        grouped_passes = {}
+
+        def turn_two_passes(g, c):
+            grouped_passes[(g, c)] = transpose_and_copy(
+                [(w_rows[g][:, h, :], c + i) for i in range(2) for h in range(HEADS)], w_permutation(g)
             )
+
+        def quantise_group(g):
+            codes, scales = w_operand[g]
+            for c in range(0, PASSES, 2):
+                quantise(
+                    grouped_passes[(g, c)],
+                    codes[:, c : c + 2, :].rearrange("p c n -> p (c n)"),
+                    scales[:, c : c + 2, :].rearrange("p c n -> p (c n)"),
+                )
+            hold_gpsimd(codes[:, PASSES - 1, :])
 
         def multiply(g, m, acc):
             codes, scales = w_operand[g]
@@ -246,9 +260,9 @@ def tile_attention_pa_kernel(tc, x, freqs_cis, wqkv, q_norm_w, k_norm_w, out_0, 
                 )
             return g, m, products
 
-        def add_and_store(g, m, products):
+        def add_and_store(g, m, products, engine):
             result = work.tile([P, HEADS * HP, 2], F32, name="result")
-            nc.gpsimd.tensor_tensor(
+            engine.tensor_tensor(
                 out=result[:], in0=products[:, 0, :, :], in1=products[:, 1, :, ::-1], op=ALU.add
             )
             store(g, m, result[:].rearrange("p n e -> p (n e)"))
@@ -279,10 +293,11 @@ def tile_attention_pa_kernel(tc, x, freqs_cis, wqkv, q_norm_w, k_norm_w, out_0, 
             acc, inv = product_and_norms(0, m)
             if m == TOKEN_TILES - 1:
                 for c in range(0, PASSES, 2):
-                    prepare_two_passes(1, c)
+                    turn_two_passes(1, c)
+                quantise_group(1)
             waiting.append(multiply_by_factors(0, m, acc, inv))
             if len(waiting) > 1:
-                add_and_store(*waiting[-2])
+                add_and_store(*waiting[-2], engine=nc.gpsimd)
 
         for g in range(1, V_GROUP):
             if g + W_BUFS < N_GROUPS:
@@ -290,11 +305,15 @@ def tile_attention_pa_kernel(tc, x, freqs_cis, wqkv, q_norm_w, k_norm_w, out_0, 
             new_w_operand(g + 1)
             for m in range(TOKEN_TILES):
                 if m < 2:
-                    prepare_two_passes(g + 1, 2 * m)
+                    turn_two_passes(g + 1, 2 * m)
                 acc, inv = product_and_norms(g, m)
+                if m == 1:
+                    quantise_group(g + 1)
+                if g == K_GROUP and m == TOKEN_TILES - 1:
+                    product_of_v(0)
                 waiting.append(multiply_by_factors(g, m, acc, inv))
-                add_and_store(*waiting[-2])
-                if g == K_GROUP and m >= 2:
-                    for v_tile in range(2 * (m - 2), 2 * (m - 2) + 2):
-                        product_of_v(v_tile)
-        add_and_store(*waiting[-1])
+                add_and_store(*waiting[-2], engine=nc.vector if m == TOKEN_TILES - 1 else nc.gpsimd)
+        product_of_v(1)
+        product_of_v(2)
+        add_and_store(*waiting[-1], engine=nc.vector)
+        product_of_v(3)

@@ -67,17 +67,20 @@ def tile_attention_pa_kernel(tc, x, freqs_cis, wqkv, q_norm_w, k_norm_w, out_0, 
 
         w_rows = {}
 
-        def load_w(g):
+        def load_w(g, column_pieces=1):
             w_rows[g] = w_pool.tile([P, HEADS, D], BF16, name="w_rows")
+            width = D // column_pieces
             for b in range(2):
                 first = GROUP * g + HALF * b
-                nc.sync.dma_start(
-                    out=w_rows[g][:, 2 * b : 2 * b + 2, :],
-                    in_=wqkv[first : first + HALF, :].rearrange("(h p) k -> p h k", p=P),
-                )
+                for i in range(column_pieces):
+                    columns = slice(width * i, width * (i + 1))
+                    nc.sync.dma_start(
+                        out=w_rows[g][:, 2 * b : 2 * b + 2, columns],
+                        in_=wqkv[first : first + HALF, columns].rearrange("(h p) k -> p h k", p=P),
+                    )
 
         load_x(0)
-        load_w(0)
+        load_w(0, column_pieces=2)
         nc.sync.dma_start(out=gain_row[0:1, 0, :], in_=q_norm_w.unsqueeze(0))
         nc.sync.dma_start(out=gain_row[0:1, 1, :], in_=k_norm_w.unsqueeze(0))
         nc.sync.dma_start(out=freqs[:], in_=freqs_cis.rearrange("(a p) j t -> p a j t", p=P))
@@ -131,7 +134,7 @@ def tile_attention_pa_kernel(tc, x, freqs_cis, wqkv, q_norm_w, k_norm_w, out_0, 
             )
             factors[(kind, a)] = table
 
-        def transpose_and_copy(pieces, permutation):
+        def transpose_and_copy(pieces, permutation, vector_banks=()):
             banks = len(pieces) // 2
             grouped = stage.tile([P, banks * HALF, PACK], BF16, align_bytes=64, name="grouped%d" % banks)
             for n in range(banks):
@@ -145,7 +148,8 @@ def tile_attention_pa_kernel(tc, x, freqs_cis, wqkv, q_norm_w, k_norm_w, out_0, 
                             in_=rows.bitcast(F32)[:, first : first + P],
                             identity=permutation,
                         )
-                nc.scalar.copy(
+                copy_out = nc.vector.tensor_copy if n in vector_banks else nc.scalar.copy
+                copy_out(
                     out=grouped[:].bitcast(F32)[:, HALF * n : HALF * (n + 1), :],
                     in_=bank[:].rearrange("p u n -> p n u"),
                 )
@@ -192,7 +196,9 @@ def tile_attention_pa_kernel(tc, x, freqs_cis, wqkv, q_norm_w, k_norm_w, out_0, 
 
         def turn_two_passes(g, c):
             grouped_passes[(g, c)] = transpose_and_copy(
-                [(w_rows[g][:, h, :], c + i) for i in range(2) for h in range(HEADS)], w_permutation(g)
+                [(w_rows[g][:, h, :], c + i) for i in range(2) for h in range(HEADS)],
+                w_permutation(g),
+                vector_banks=(3,) if c == 0 else (),
             )
 
         def quantise_group(g):
@@ -312,7 +318,8 @@ def tile_attention_pa_kernel(tc, x, freqs_cis, wqkv, q_norm_w, k_norm_w, out_0, 
                 if g == K_GROUP and m == TOKEN_TILES - 1:
                     product_of_v(0)
                 waiting.append(multiply_by_factors(g, m, acc, inv))
-                add_and_store(*waiting[-2], engine=nc.vector if m == TOKEN_TILES - 1 else nc.gpsimd)
+                last_of_k = g == K_GROUP and m == TOKEN_TILES - 1
+                add_and_store(*waiting[-2], engine=nc.vector if last_of_k else nc.gpsimd)
         product_of_v(1)
         product_of_v(2)
         add_and_store(*waiting[-1], engine=nc.vector)

@@ -15,7 +15,6 @@ P = 128
 PACK = 4
 K_PASS = P * PACK
 WORDS_PASS = K_PASS // 2
-
 TOKENS = 512
 D = 2048
 PASSES = D // K_PASS
@@ -29,24 +28,26 @@ Q_GROUPS = 4
 K_GROUP = 4
 V_GROUP = 5
 N_GROUPS = 6
-W_BUFS = 3
 EPS = 1e-6
-
 FLOPS = 2 * TOKENS * D * (N_GROUPS * GROUP)
+
+KNOBS = dict(W_BUFS=3, head_v=(), last_add_v=0, variant='C',res_bufs=8,w0_split=2,seq0='MM0 SQ0 STT0 MM1 SQ1 STT1 ADD0 MM2 SQ2 STT2 ADD1 MM3 SQ3 UA UB QA QB HB STT3 ADD2',seq1='UA MM0 SQ0 STT0 ADDp UB MM1 SQ1 QA QB HB STT1 ADD0 NAa MM2 SQ2 STT2 ADD1 NAb MM3 SQ3 STT3 ADD2',seq='UBa MM0 SQ0 STT0 ADDp UBb MM1 SQ1 QA QB HB STT1 ADD0 NAa MM2 SQ2 STT2 ADD1 NAb MM3 SQ3 STT3 ADD2',seqk='UBa MM0 SQ0 STT0 ADDp UBb MM1 SQ1 QA QB HB STT1 ADD0 MM2 SQ2 STT2 ADD1 MM3 SQ3 VM0 VC0 STT3 ADD2v VM1 VC1 VM2 VC2 ADD3v VM3 VC3',vshare=((),(1,)))
 
 
 def tile_attention_pa_kernel(tc, x, freqs_cis, wqkv, q_norm_w, k_norm_w, out_0, out_1, out_2):
     nc = tc.nc
+    K = KNOBS
+    W_BUFS = K['W_BUFS']
     with ExitStack() as ctx:
         const = ctx.enter_context(tc.tile_pool(name="const", bufs=1))
         w_pool = ctx.enter_context(tc.tile_pool(name="w_pool", bufs=W_BUFS))
-        stage = ctx.enter_context(tc.tile_pool(name="stage", bufs=4))
-        quantised = ctx.enter_context(tc.tile_pool(name="quantised", bufs=2))
+        stage = ctx.enter_context(tc.tile_pool(name="stage", bufs=3))
+        quantised = ctx.enter_context(tc.tile_pool(name="quantised", bufs=K.get('q_bufs', 5)))
         work = ctx.enter_context(tc.tile_pool(name="work", bufs=4))
+        results = ctx.enter_context(tc.tile_pool(name="results", bufs=K['res_bufs']))
         small = ctx.enter_context(tc.tile_pool(name="small", bufs=4))
-        t_psum = ctx.enter_context(tc.psum_pool(name="t_psum", bufs=4))
-        acc_psum = ctx.enter_context(tc.psum_pool(name="acc_psum", bufs=4))
-
+        t_psum = ctx.enter_context(tc.psum_pool(name="t_psum", bufs=K.get('t_banks', 4)))
+        acc_psum = ctx.enter_context(tc.psum_pool(name="acc_psum", bufs=8 - K.get('t_banks', 4)))
         ctx.enter_context(tc.manual_schedule())
 
         x_rows_dram = x.rearrange("b s k -> (b s) k")
@@ -59,35 +60,32 @@ def tile_attention_pa_kernel(tc, x, freqs_cis, wqkv, q_norm_w, k_norm_w, out_0, 
         gain_row = const.tile([P, 2, HD], BF16, name="gain_row")
         nc.vector.memset(gain_row[:], 0.0)
         freqs = const.tile([P, 2, HP, 2], BF16, name="freqs")
-
         x_rows = const.tile([P, TOKEN_TILES, D], BF16, name="x_rows")
 
         def load_x(m):
-            nc.sync.dma_start(out=x_rows[:, m, :], in_=x_rows_dram[P * m : P * (m + 1), :])
+            n = K.get('x_split', 1) if m == 0 else 1
+            w = D // n
+            for i in range(n):
+                nc.sync.dma_start(out=x_rows[:, m, w * i : w * (i + 1)], in_=x_rows_dram[P * m : P * (m + 1), w * i : w * (i + 1)])
 
         w_rows = {}
 
-        def load_w(g, column_pieces=1):
+        def load_w(g):
             w_rows[g] = w_pool.tile([P, HEADS, D], BF16, name="w_rows")
-            width = D // column_pieces
+            n = K.get('w0_split', 1) if g == 0 else 1
+            w = D // n
             for b in range(2):
                 first = GROUP * g + HALF * b
-                for i in range(column_pieces):
-                    columns = slice(width * i, width * (i + 1))
+                for i in range(n):
                     nc.sync.dma_start(
-                        out=w_rows[g][:, 2 * b : 2 * b + 2, columns],
-                        in_=wqkv[first : first + HALF, columns].rearrange("(h p) k -> p h k", p=P),
+                        out=w_rows[g][:, 2 * b : 2 * b + 2, w * i : w * (i + 1)],
+                        in_=wqkv[first : first + HALF, w * i : w * (i + 1)].rearrange("(h p) k -> p h k", p=P),
                     )
 
-        load_x(0)
-        load_w(0, column_pieces=2)
-        nc.sync.dma_start(out=gain_row[0:1, 0, :], in_=q_norm_w.unsqueeze(0))
-        nc.sync.dma_start(out=gain_row[0:1, 1, :], in_=k_norm_w.unsqueeze(0))
-        nc.sync.dma_start(out=freqs[:], in_=freqs_cis.rearrange("(a p) j t -> p a j t", p=P))
-        for m in range(1, TOKEN_TILES):
-            load_x(m)
-        for g in range(1, W_BUFS):
-            load_w(g)
+        def load_small():
+            nc.sync.dma_start(out=gain_row[0:1, 0, :], in_=q_norm_w.unsqueeze(0))
+            nc.sync.dma_start(out=gain_row[0:1, 1, :], in_=k_norm_w.unsqueeze(0))
+            nc.sync.dma_start(out=freqs[:], in_=freqs_cis.rearrange("(a p) j t -> p a j t", p=P))
 
         eps = const.tile([P, 1], F32, name="eps")
         nc.vector.memset(eps[:], EPS)
@@ -97,17 +95,12 @@ def tile_attention_pa_kernel(tc, x, freqs_cis, wqkv, q_norm_w, k_norm_w, out_0, 
         nc.vector.memset(ones[:], 1.0)
         ident = const.tile([P, P], F32, name="ident")
         make_identity(nc, ident[:])
-
         gains = const.tile([P, 2, HP, 2], F32, name="gains")
 
         def spread_gains():
             gain_bank = t_psum.tile([P, 2, HALF], F32, name="bank")
             nc.tensor.matmul(
-                out=gain_bank[:, 0, :],
-                lhsT=ones[:],
-                rhs=gain_row[:].rearrange("p a d -> p (a d)"),
-                start=True,
-                stop=True,
+                out=gain_bank[:, 0, :], lhsT=ones[:], rhs=gain_row[:].rearrange("p a d -> p (a d)"), start=True, stop=True
             )
             nc.scalar.copy(out=gains[:].rearrange("p a j e -> p (a j e)"), in_=gain_bank[:, 0, :])
 
@@ -134,92 +127,121 @@ def tile_attention_pa_kernel(tc, x, freqs_cis, wqkv, q_norm_w, k_norm_w, out_0, 
             )
             factors[(kind, a)] = table
 
-        def transpose_and_copy(pieces, permutation, vector_banks=()):
+        units = {}
+
+        def new_unit(key, pieces, codes, scales):
             banks = len(pieces) // 2
             grouped = stage.tile([P, banks * HALF, PACK], BF16, align_bytes=64, name="grouped%d" % banks)
-            for n in range(banks):
-                bank = t_psum.tile([P, 2, HALF], F32, name="bank")
-                for u in range(2):
-                    for i in range(2):
-                        rows, c = pieces[2 * n + i]
-                        first = WORDS_PASS * c + P * u
-                        nc.tensor.transpose(
-                            out=bank[:, u, P * i : P * (i + 1)],
-                            in_=rows.bitcast(F32)[:, first : first + P],
-                            identity=permutation,
-                        )
-                copy_out = nc.vector.tensor_copy if n in vector_banks else nc.scalar.copy
-                copy_out(
-                    out=grouped[:].bitcast(F32)[:, HALF * n : HALF * (n + 1), :],
-                    in_=bank[:].rearrange("p u n -> p n u"),
-                )
-            return grouped
+            units[key] = dict(pieces=pieces, codes=codes, scales=scales, grouped=grouped, banks={})
 
-        def quantise(grouped, codes, scales):
+        def unit_T(key, n):
+            u = units[key]
+            bank = t_psum.tile([P, 2, HALF], F32, name="bank")
+            u['banks'][n] = bank
+            for uu in range(2):
+                for i in range(2):
+                    rows, c = u['pieces'][2 * n + i]
+                    first = WORDS_PASS * c + P * uu
+                    nc.tensor.transpose(
+                        out=bank[:, uu, P * i : P * (i + 1)], in_=rows.bitcast(F32)[:, first : first + P], identity=ident[:]
+                    )
+
+        def unit_C(key, n, on_vector):
+            u = units[key]
+            dst = u['grouped'][:].bitcast(F32)[:, HALF * n : HALF * (n + 1), :]
+            src = u['banks'][n][:].rearrange("p u n -> p n u")
+            if on_vector:
+                nc.vector.tensor_copy(out=dst, in_=src)
+            else:
+                nc.scalar.copy(out=dst, in_=src)
+
+        def unit_Q(key):
+            u = units[key]
             nc.vector.quantize_mx(
-                out=codes.bitcast(FP8X4), scales=scales, in_=grouped[:].rearrange("p n t -> p (n t)")
+                out=u['codes'].bitcast(FP8X4), scales=u['scales'], in_=u['grouped'][:].rearrange("p n t -> p (n t)")
             )
 
-        def prepare(pieces, permutation, codes, scales):
-            quantise(transpose_and_copy(pieces, permutation), codes, scales)
-
-        def hold_gpsimd(codes):
+        def unit_H(key):
             held = small.tile([P, 1], U32, name="held")
-            nc.gpsimd.tensor_copy(out=held[:], in_=codes[:, 0:1])
+            nc.gpsimd.tensor_copy(out=held[:], in_=units[key]['codes'][:, 0:1])
 
         x_codes = const.tile([P, TOKEN_TILES, PASSES * P], U32, align_bytes=64, name="x_codes")
         x_scales = const.tile([P, TOKEN_TILES, PASSES * P], U8, align_bytes=64, name="x_scales")
-
-        def prepare_x(m):
-            prepare([(x_rows[:, m, :], c) for c in range(PASSES)], ident[:], x_codes[:, m, :], x_scales[:, m, :])
-
         w_operand = {}
 
-        def new_w_operand(g):
-            codes = quantised.tile([P, PASSES, GROUP], U32, align_bytes=64, name="w_codes")
-            scales = quantised.tile([P, PASSES, GROUP], U8, align_bytes=64, name="w_scales")
-            w_operand[g] = (codes, scales)
+        def new_w_half(g, half):
+            codes = quantised.tile([P, 2, GROUP], U32, align_bytes=64, name="w_codes")
+            scales = quantised.tile([P, 2, GROUP], U8, align_bytes=64, name="w_scales")
+            w_operand[(g, half)] = (codes, scales)
 
-        def w_permutation(g):
-            return ident[:]
+        def make_x_unit(m):
+            new_unit(('x', m), [(x_rows[:, m, :], c) for c in range(PASSES)], x_codes[:, m, :], x_scales[:, m, :])
 
-        def prepare_half_pass(g, c, b):
-            codes, scales = w_operand[g]
-            prepare(
-                [(w_rows[g][:, 2 * b + i, :], c) for i in range(2)],
-                w_permutation(g),
-                codes[:, c, HALF * b : HALF * (b + 1)],
-                scales[:, c, HALF * b : HALF * (b + 1)],
+        def make_w_unit(g, half):
+            new_w_half(g, half)
+            codes, scales = w_operand[(g, half)]
+            new_unit(
+                ('w', g, half),
+                [(w_rows[g][:, h, :], 2 * half + i) for i in range(2) for h in range(HEADS)],
+                codes[:].rearrange("p c n -> p (c n)"),
+                scales[:].rearrange("p c n -> p (c n)"),
             )
 
-        grouped_passes = {}
-
-        def turn_two_passes(g, c):
-            grouped_passes[(g, c)] = transpose_and_copy(
-                [(w_rows[g][:, h, :], c + i) for i in range(2) for h in range(HEADS)],
-                w_permutation(g),
-                vector_banks=(3,) if c == 0 else (),
+        def make_w0_unit(c, b):
+            codes, scales = w_operand[(0, c // 2)]
+            new_unit(
+                ('w0', c, b),
+                [(w_rows[0][:, 2 * b + i, :], c) for i in range(2)],
+                codes[:, c % 2, HALF * b : HALF * (b + 1)],
+                scales[:, c % 2, HALF * b : HALF * (b + 1)],
             )
 
-        def quantise_group(g):
-            codes, scales = w_operand[g]
-            for c in range(0, PASSES, 2):
-                quantise(
-                    grouped_passes[(g, c)],
-                    codes[:, c : c + 2, :].rearrange("p c n -> p (c n)"),
-                    scales[:, c : c + 2, :].rearrange("p c n -> p (c n)"),
-                )
-            hold_gpsimd(codes[:, PASSES - 1, :])
+        def make_w0_half_unit(b):
+            codes = quantised.tile([P, PASSES, HALF], U32, align_bytes=64, name="w_codes")
+            scales = quantised.tile([P, PASSES, HALF], U8, align_bytes=64, name="w_scales")
+            w_operand[('h', b)] = (codes, scales)
+            new_unit(
+                ('w0h', b),
+                [(w_rows[0][:, 2 * b + i, :], c) for c in range(PASSES) for i in range(2)],
+                codes[:].rearrange("p c n -> p (c n)"),
+                scales[:].rearrange("p c n -> p (c n)"),
+            )
 
-        def multiply(g, m, acc):
-            codes, scales = w_operand[g]
+        accs = {}
+        invs = {}
+        prods = {}
+        pair_tiles = {}
+
+        def MM(g, m):
+            if g == V_GROUP and K.get('v_in_t', True):
+                acc = t_psum.tile([P, 2, HALF], F32, name="bank")
+                flat = acc[:].rearrange("p u n -> p (u n)")
+            else:
+                acc = acc_psum.tile([P, HEADS, HD], F32, name="acc")
+                flat = acc[:].rearrange("p h d -> p (h d)")
+            accs[(g, m)] = (acc, flat)
+            if g == 0 and K.get('w0_halves'):
+                for b in range(2):
+                    codes, scales = w_operand[('h', b)]
+                    for c in range(PASSES):
+                        nc.tensor.matmul_mx(
+                            out=flat[:, HALF * b : HALF * (b + 1)],
+                            lhsT=x_codes[:, m, P * c : P * (c + 1)].bitcast(FP8X4),
+                            lhsT_scale=x_scales[:, m, P * c : P * (c + 1)],
+                            rhs=codes[:, c, :].bitcast(FP8X4),
+                            rhs_scale=scales[:, c, :],
+                            start=(c == 0),
+                            stop=(c == PASSES - 1),
+                        )
+                return
             for c in range(PASSES):
+                codes, scales = w_operand[(g, c // 2)]
                 nc.tensor.matmul_mx(
-                    out=acc,
+                    out=flat,
                     lhsT=x_codes[:, m, P * c : P * (c + 1)].bitcast(FP8X4),
                     lhsT_scale=x_scales[:, m, P * c : P * (c + 1)],
-                    rhs=codes[:, c, :].bitcast(FP8X4),
-                    rhs_scale=scales[:, c, :],
+                    rhs=codes[:, c % 2, :].bitcast(FP8X4),
+                    rhs_scale=scales[:, c % 2, :],
                     start=(c == 0),
                     stop=(c == PASSES - 1),
                 )
@@ -233,28 +255,28 @@ def tile_attention_pa_kernel(tc, x, freqs_cis, wqkv, q_norm_w, k_norm_w, out_0, 
                 dst = out_dram[2][P * m : P * (m + 1), :]
             nc.sync.dma_start(out=dst, in_=result)
 
-        def product_and_norms(g, m):
-            acc = acc_psum.tile([P, HEADS, HD], F32, name="acc")
-            multiply(g, m, acc[:].rearrange("p h d -> p (h d)"))
+        def SQ(g, m):
+            acc = accs[(g, m)][0]
             sumsq = small.tile([P, HEADS], F32, name="sumsq")
             for h in range(HEADS):
                 squares = small.tile([P, HD], BF16, name="squares")
-                nc.scalar.activation(
-                    out=squares[:],
-                    in_=acc[:, h, :],
-                    func=ACT.Square,
-                    accum_out=sumsq[:, h : h + 1],
-                )
+                nc.scalar.activation(out=squares[:], in_=acc[:, h, :], func=ACT.Square, accum_out=sumsq[:, h : h + 1])
             inv = small.tile([P, HEADS], F32, name="inv")
-            nc.scalar.activation(
-                out=inv[:], in_=sumsq[:], func=ACT.Abs_reciprocal_sqrt, bias=eps[:, 0:1], scale=1.0 / HD
-            )
-            return acc, inv
+            nc.scalar.activation(out=inv[:], in_=sumsq[:], func=ACT.Abs_reciprocal_sqrt, bias=eps[:, 0:1], scale=1.0 / HD)
+            invs[(g, m)] = inv
 
-        def multiply_by_factors(g, m, acc, inv):
-            kind = 0 if g < Q_GROUPS else 1
-            table = factors[(kind, m % 2)]
-            products = work.tile([P, 2, HEADS * HP, 2], F32, name="products")
+        def STT(g, m):
+            acc = accs[(g, m)][0]
+            inv = invs[(g, m)]
+            table = factors[(0 if g < Q_GROUPS else 1, m % 2)]
+            if K.get('pairs'):
+                bank_no = TOKEN_TILES * g + m + K.get('pair_shift', 0)
+                if bank_no // 2 not in pair_tiles:
+                    pair_tiles[bank_no // 2] = (work.tile([P, 2, 2, HEADS * HP, 2], F32, name="products2"), [])
+                pair_tiles[bank_no // 2][1].append((bank_no % 2, g, m))
+                products = pair_tiles[bank_no // 2][0][:, bank_no % 2, :, :, :]
+            else:
+                products = work.tile([P, 2, HEADS * HP, 2], F32, name="products")
             for h in range(HEADS):
                 nc.vector.scalar_tensor_tensor(
                     out=products[:, :, HP * h : HP * (h + 1), :].rearrange("p k j e -> p k (j e)"),
@@ -264,63 +286,290 @@ def tile_attention_pa_kernel(tc, x, freqs_cis, wqkv, q_norm_w, k_norm_w, out_0, 
                     op0=ALU.mult,
                     op1=ALU.mult,
                 )
-            return g, m, products
+            prods[(g, m)] = products
 
-        def add_and_store(g, m, products, engine):
-            result = work.tile([P, HEADS * HP, 2], F32, name="result")
-            engine.tensor_tensor(
-                out=result[:], in0=products[:, 0, :, :], in1=products[:, 1, :, ::-1], op=ALU.add
-            )
+        def ADD(g, m, on_vector=False):
+            products = prods[(g, m)]
+            result = results.tile([P, HEADS * HP, 2], F32, name="result")
+            eng = nc.vector if on_vector else nc.gpsimd
+            eng.tensor_tensor(out=result[:], in0=products[:, 0, :, :], in1=products[:, 1, :, ::-1], op=ALU.add)
             store(g, m, result[:].rearrange("p n e -> p (n e)"))
 
-        def product_of_v(m):
-            acc = t_psum.tile([P, 2, HALF], F32, name="bank")
-            multiply(V_GROUP, m, acc[:].rearrange("p u n -> p (u n)"))
-            v_result = work.tile([P, GROUP], F32, name="v_result")
-            nc.scalar.copy(out=v_result[:], in_=acc[:].rearrange("p u n -> p (u n)"))
+        def ADD2(g, pair, on_vector=False):
+            prod, members = pair_tiles[(TOKEN_TILES * g + pair + K.get('pair_shift', 0)) // 2]
+            result = results.tile([P, 2, HEADS * HP, 2], F32, name="result2")
+            eng = nc.vector if on_vector else nc.gpsimd
+            lo = min(member[0] for member in members)
+            hi = max(member[0] for member in members) + 1
+            eng.tensor_tensor(
+                out=result[:, lo:hi, :, :], in0=prod[:, lo:hi, 0, :, :], in1=prod[:, lo:hi, 1, :, ::-1], op=ALU.add
+            )
+            for s, gg, mm in members:
+                store(gg, mm, result[:, s, :, :].rearrange("p n e -> p (n e)"))
+
+        def VC(m):
+            flat = accs[(V_GROUP, m)][1]
+            v_result = results.tile([P, GROUP], F32, name="result")
+            nc.scalar.copy(out=v_result[:], in_=flat)
             store(V_GROUP, m, v_result[:])
 
-        new_w_operand(0)
-        prepare_x(0)
-        for b in range(2):
-            for c in range(PASSES):
-                prepare_half_pass(0, c, b)
-        spread_gains()
+        ORDER(K, dict(load_x=load_x, load_w=load_w, load_small=load_small, spread_gains=spread_gains,
+                      make_factors=make_factors, make_x_unit=make_x_unit, make_w_unit=make_w_unit,
+                      make_w0_unit=make_w0_unit, make_w0_half_unit=make_w0_half_unit, new_w_half=new_w_half, T=unit_T, C=unit_C, Q=unit_Q, H=unit_H,
+                      MM=MM, SQ=SQ, STT=STT, ADD=ADD, ADD2=ADD2, VC=VC))
+
+
+def ORDER(K, f):
+    W_BUFS = K['W_BUFS']
+    f['load_x'](0)
+    if K.get('small_first'):
+        f['load_small']()
+    f['load_w'](0)
+    if not K.get('small_first'):
+        f['load_small']()
+    if K.get('w1_early'):
+        f['load_x'](1)
+        f['load_w'](1)
+        f['load_x'](2)
+        f['load_x'](3)
+        for g in range(2, W_BUFS):
+            f['load_w'](g)
+    else:
         for m in range(1, TOKEN_TILES):
-            prepare_x(m)
+            f['load_x'](m)
+        for g in range(1, W_BUFS):
+            f['load_w'](g)
+    if K['variant'] == 'A':
+        order_A(K, f)
+    elif K['variant'] == 'B':
+        order_B(K, f)
+    else:
+        order_C(K, f)
+
+
+def whole_unit(f, key, banks, vset=()):
+    for n in range(banks):
+        f['T'](key, n)
+        f['C'](key, n, n in vset)
+    f['Q'](key)
+
+
+def order_A(K, f):
+    W_BUFS = K['W_BUFS']
+    f['new_w_half'](0, 0)
+    f['new_w_half'](0, 1)
+    f['make_x_unit'](0)
+    whole_unit(f, ('x', 0), 2, K.get('hx', ()))
+    for b in range(2):
+        for c in range(PASSES):
+            f['make_w0_unit'](c, b)
+            whole_unit(f, ('w0', c, b), 1, (0,) if (b, c) in K['head_v'] else ())
+    f['spread_gains']()
+    for m in range(1, TOKEN_TILES):
+        f['make_x_unit'](m)
+        whole_unit(f, ('x', m), 2, K.get('hx', ()))
+    for kind in range(2):
+        for a in range(2):
+            f['make_factors'](kind, a)
+    if W_BUFS < N_GROUPS:
+        f['load_w'](W_BUFS)
+    waiting = []
+    for m in range(TOKEN_TILES):
+        f['MM'](0, m)
+        f['SQ'](0, m)
+        if m == TOKEN_TILES - 1:
+            for half in range(2):
+                f['make_w_unit'](1, half)
+                whole_unit(f, ('w', 1, half), 4, K['vshare'][half])
+        f['STT'](0, m)
+        waiting.append((0, m))
+        if len(waiting) > 1:
+            f['ADD'](*waiting[-2])
+    for g in range(1, V_GROUP):
+        if W_BUFS <= g + W_BUFS < N_GROUPS:
+            f['load_w'](g + W_BUFS)
+        for m in range(TOKEN_TILES):
+            if m < 2:
+                f['make_w_unit'](g + 1, m)
+                whole_unit(f, ('w', g + 1, m), 4, K['vshare'][m])
+            f['MM'](g, m)
+            f['SQ'](g, m)
+            f['STT'](g, m)
+            waiting.append((g, m))
+            f['ADD'](*waiting[-2])
+            if g == K_GROUP and m >= 2:
+                for v_tile in range(2 * (m - 2), 2 * (m - 2) + 2):
+                    f['MM'](V_GROUP, v_tile)
+                    f['VC'](v_tile)
+    f['ADD'](*waiting[-1], on_vector=bool(K['last_add_v']))
+
+
+def order_B(K, f):
+    W_BUFS = K['W_BUFS']
+    f['new_w_half'](0, 0)
+    f['new_w_half'](0, 1)
+    f['make_x_unit'](0)
+    whole_unit(f, ('x', 0), 2, K.get('hx0', ()))
+
+    def tables():
+        f['spread_gains']()
         for kind in range(2):
             for a in range(2):
-                make_factors(kind, a)
+                f['make_factors'](kind, a)
 
-        load_w(W_BUFS)
-        new_w_operand(1)
-        waiting = []
+    if K.get('small_first'):
+        tables()
+    for b in range(2):
+        for c in range(PASSES):
+            f['make_w0_unit'](c, b)
+            whole_unit(f, ('w0', c, b), 1, (0,) if (b, c) in K['head_v'] else ())
+    if not K.get('small_first'):
+        tables()
+    if W_BUFS < N_GROUPS:
+        f['load_w'](W_BUFS)
+    waiting = []
+    xa = K.get('x_ahead', 1)
+    for m in range(1, 1 + xa):
+        f['make_x_unit'](m)
+        whole_unit(f, ('x', m), 2, K.get('hx', ()))
+    for m in range(TOKEN_TILES):
+        f['MM'](0, m)
+        if m + 1 + xa < TOKEN_TILES + 1 and m + xa + 1 <= TOKEN_TILES - 1:
+            f['make_x_unit'](m + xa + 1)
+            whole_unit(f, ('x', m + xa + 1), 2, K.get('hx', ()))
+        f['SQ'](0, m)
+        if m == K.get('w1_at', TOKEN_TILES - 1):
+            for half in range(2):
+                f['make_w_unit'](1, half)
+                whole_unit(f, ('w', 1, half), 4, K.get('vshare1', K['vshare'])[half])
+        f['STT'](0, m)
+        waiting.append((0, m))
+        if len(waiting) > 1:
+            f['ADD'](*waiting[-2])
+    for g in range(1, V_GROUP):
+        if W_BUFS <= g + W_BUFS < N_GROUPS:
+            f['load_w'](g + W_BUFS)
         for m in range(TOKEN_TILES):
-            acc, inv = product_and_norms(0, m)
-            if m == TOKEN_TILES - 1:
-                for c in range(0, PASSES, 2):
-                    turn_two_passes(1, c)
-                quantise_group(1)
-            waiting.append(multiply_by_factors(0, m, acc, inv))
-            if len(waiting) > 1:
-                add_and_store(*waiting[-2], engine=nc.gpsimd)
+            if m < 2:
+                f['make_w_unit'](g + 1, m)
+                whole_unit(f, ('w', g + 1, m), 4, K['vshare'][m])
+            f['MM'](g, m)
+            f['SQ'](g, m)
+            f['STT'](g, m)
+            waiting.append((g, m))
+            f['ADD'](*waiting[-2])
+            if g == K_GROUP and not K.get('v_last') and m >= 2:
+                for v_tile in range(2 * (m - 2), 2 * (m - 2) + 2):
+                    f['MM'](V_GROUP, v_tile)
+                    f['VC'](v_tile)
+    if K.get('v_last'):
+        f['ADD'](*waiting[-1], on_vector=bool(K['last_add_v']))
+        for v_tile in range(TOKEN_TILES):
+            f['MM'](V_GROUP, v_tile)
+            f['VC'](v_tile)
+    else:
+        f['ADD'](*waiting[-1], on_vector=bool(K['last_add_v']))
 
-        for g in range(1, V_GROUP):
-            if g + W_BUFS < N_GROUPS:
-                load_w(g + W_BUFS)
-            new_w_operand(g + 1)
-            for m in range(TOKEN_TILES):
-                if m < 2:
-                    turn_two_passes(g + 1, 2 * m)
-                acc, inv = product_and_norms(g, m)
-                if m == 1:
-                    quantise_group(g + 1)
-                if g == K_GROUP and m == TOKEN_TILES - 1:
-                    product_of_v(0)
-                waiting.append(multiply_by_factors(g, m, acc, inv))
-                last_of_k = g == K_GROUP and m == TOKEN_TILES - 1
-                add_and_store(*waiting[-2], engine=nc.vector if last_of_k else nc.gpsimd)
-        product_of_v(1)
-        product_of_v(2)
-        add_and_store(*waiting[-1], engine=nc.vector)
-        product_of_v(3)
+
+def run_seq(K, f, g, seq, prev):
+    for tok in seq.split():
+        if tok in ('UA', 'UB'):
+            half = 0 if tok == 'UA' else 1
+            if g + 1 > V_GROUP: continue
+            f['make_w_unit'](g + 1, half)
+            for n in range(4):
+                f['T'](('w', g + 1, half), n)
+                f['C'](('w', g + 1, half), n, n in K.get('vshare_g', {}).get(g + 1, K['vshare'])[half])
+        elif tok in ('UAa', 'UAb', 'UBa', 'UBb'):
+            half = 0 if tok[1] == 'A' else 1
+            if g + 1 > V_GROUP: continue
+            if tok[2] == 'a':
+                f['make_w_unit'](g + 1, half)
+            for n in ((0, 1) if tok[2] == 'a' else (2, 3)):
+                f['T'](('w', g + 1, half), n)
+                f['C'](('w', g + 1, half), n, n in K.get('vshare_g', {}).get(g + 1, K['vshare'])[half])
+        elif tok in ('NAa', 'NAb'):
+            if g + 2 > V_GROUP: continue
+            if tok[2] == 'a':
+                f['make_w_unit'](g + 2, 0)
+            for n in ((0, 1) if tok[2] == 'a' else (2, 3)):
+                f['T'](('w', g + 2, 0), n)
+                f['C'](('w', g + 2, 0), n, n in K.get('vshare_n', ()))
+        elif tok in ('QA', 'QB'):
+            if g + 1 > V_GROUP: continue
+            f['Q'](('w', g + 1, 0 if tok == 'QA' else 1))
+        elif tok in ('HA', 'HB'):
+            if g + 1 > V_GROUP: continue
+            f['H'](('w', g + 1, 0 if tok == 'HA' else 1))
+        elif tok.startswith('MM'):
+            f['MM'](g, int(tok[2:]))
+        elif tok.startswith('SQ'):
+            f['SQ'](g, int(tok[2:]))
+        elif tok.startswith('STT'):
+            f['STT'](g, int(tok[3:]))
+        elif tok.startswith('ADDW'):
+            f['ADD2'](g, int(tok[4]), on_vector=tok[-1] == 'v')
+        elif tok.startswith('ADDp'):
+            if prev is not None: f['ADD'](*prev, on_vector=tok[-1] == 'v')
+        elif tok.startswith('ADD'):
+            f['ADD'](g, int(tok[3]), on_vector=tok[-1] == 'v')
+        elif tok.startswith('VM'):
+            f['MM'](V_GROUP, int(tok[2:]))
+        elif tok.startswith('VC'):
+            f['VC'](int(tok[2:]))
+        elif tok.startswith('X'):
+            m = int(tok[1:])
+            f['make_x_unit'](m)
+            whole_unit(f, ('x', m), 2, K.get('hx', ()))
+        else:
+            raise ValueError(tok)
+
+
+SEQ06 = "UA QA HA MM0 SQ0 STT0 ADDp UB QB HB MM1 SQ1 STT1 ADD0 MM2 SQ2 STT2 ADD1 MM3 SQ3 STT3 ADD2"
+SEQ0 = "MM0 SQ0 STT0 MM1 SQ1 STT1 ADD0 MM2 SQ2 STT2 ADD1 MM3 SQ3 UA QA HA UB QB HB STT3 ADD2"
+SEQK = "MM0 SQ0 STT0 ADDp MM1 SQ1 STT1 ADD0 MM2 SQ2 STT2 ADD1 VM0 VC0 VM1 VC1 MM3 SQ3 STT3 ADD2 VM2 VC2 VM3 VC3 ADD3"
+
+
+def order_C(K, f):
+    W_BUFS = K['W_BUFS']
+    if not K.get('w0_halves'):
+        f['new_w_half'](0, 0)
+        f['new_w_half'](0, 1)
+    f['make_x_unit'](0)
+    whole_unit(f, ('x', 0), 2, K.get('hx0', ()))
+
+    def tables():
+        f['spread_gains']()
+        for kind in range(2):
+            for a in range(2):
+                f['make_factors'](kind, a)
+
+    if K.get('small_first'):
+        tables()
+    for b in range(2):
+        if K.get('w0_halves'):
+            f['make_w0_half_unit'](b)
+            whole_unit(f, ('w0h', b), 4, K.get('w0h_v', ()))
+            continue
+        for c in range(PASSES):
+            f['make_w0_unit'](c, b)
+            whole_unit(f, ('w0', c, b), 1, (0,) if (b, c) in K['head_v'] else ())
+    if not K.get('small_first') and not K.get('tables_late'):
+        f['spread_gains']()
+    run_seq(K, f, 0, K.get('seqx', 'X1 X2 X3'), None)
+    if not K.get('small_first'):
+        if K.get('tables_late'):
+            f['spread_gains']()
+        for kind in range(2):
+            for a in range(2):
+                f['make_factors'](kind, a)
+    if W_BUFS < N_GROUPS:
+        f['load_w'](W_BUFS)
+    run_seq(K, f, 0, K.get('seq0', SEQ0), None)
+    for g in range(1, V_GROUP):
+        if W_BUFS <= g + W_BUFS < N_GROUPS:
+            f['load_w'](g + W_BUFS)
+        if g < K_GROUP:
+            run_seq(K, f, g, K.get('seq1', K.get('seq', SEQ06)) if g == 1 else K.get('seq', SEQ06), (g - 1, 3))
+        else:
+            run_seq(K, f, g, K.get('seqk', "UA QA HA " + SEQK.replace("MM1", "UB QB HB MM1")), (g - 1, 3))

@@ -30,24 +30,41 @@ V_GROUP = 5
 N_GROUPS = 6
 EPS = 1e-6
 FLOPS = 2 * TOKENS * D * (N_GROUPS * GROUP)
+DUMMY = 320
 
-KNOBS = dict(W_BUFS=3, head_v=(), last_add_v=0, variant='C',res_bufs=8,w0_split=2,seq0='MM0 SQ0 STT0 MM1 SQ1 STT1 ADD0 MM2 SQ2 STT2 ADD1 MM3 SQ3 UA UB QA QB HB STT3 ADD2',seq1='UA MM0 SQ0 STT0 ADDp UB MM1 SQ1 QA QB HB STT1 ADD0 NAa MM2 SQ2 STT2 ADD1 NAb MM3 SQ3 STT3 ADD2',seq='UBa MM0 SQ0 STT0 ADDp UBb MM1 SQ1 QA QB HB STT1 ADD0 NAa MM2 SQ2 STT2 ADD1 NAb MM3 SQ3 STT3 ADD2',seqk='UBa MM0 SQ0 STT0 ADDp UBb MM1 SQ1 QA QB HB STT1 ADD0 MM2 SQ2 STT2 ADD1 MM3 SQ3 VM0 VC0 STT3 ADD2v VM1 VC1 VM2 VC2 ADD3v VM3 VC3',vshare=((),(1,)))
+PROGRAM = """
+LX:0 LW:0:q LS:s LX:1 LX:2 LX:3 LW:1:b LW:2:b P:x0 K:x0:0:s P:x0 K:x0:1:s Q:x0 P:u00 K:u00:0:s Q:u00
+P:u10 K:u10:0:s Q:u10 P:u20 K:u20:0:s Q:u20 P:u30 K:u30:0:s Q:u30 P:u01 K:u01:0:s Q:u01 P:u11 K:u11:0:s
+Q:u11 P:u21 K:u21:0:s Q:u21 P:u31 K:u31:0:s Q:u31 G P:x1 K:x1:0:s P:x1 K:x1:1:s Q:x1 P:x2 K:x2:0:s P:x2
+K:x2:1:s Q:x2 P:x3 K:x3:0:s P:x3 K:x3:1:s Q:x3 F:00 F:01 F:10 F:11 LW:3:b M:00 S:00 I:00 R:00 M:01 S:01
+I:01 R:01 A:00 M:02 S:02 I:02 R:02 A:01 M:03 S:03 I:03 P:w10 K:w10:0:s P:w10 K:w10:1:s P:w10 K:w10:2:s
+P:w10 K:w10:3:s P:w11 K:w11:0:s P:w11 K:w11:1:v P:w11 K:w11:2:s P:w11 K:w11:3:s Q:w10 Q:w11 H:w11 R:03
+A:02 LW:4:b P:w20 K:w20:0:s P:w20 K:w20:1:s P:w20 K:w20:2:s P:w20 K:w20:3:s M:10 S:10 I:10 R:10 A:03
+P:w21 K:w21:0:s P:w21 K:w21:1:v P:w21 K:w21:2:s P:w21 K:w21:3:s M:11 S:11 I:11 Q:w20 Q:w21 H:w21 R:11
+A:10 P:w30 K:w30:0:s P:w30 K:w30:1:s M:12 S:12 I:12 R:12 A:11 P:w30 K:w30:2:s P:w30 K:w30:3:s M:13 S:13
+I:13 R:13 A:12 LW:5:b P:w31 K:w31:0:s P:w31 K:w31:1:v M:20 S:20 I:20 R:20 A:13 P:w31 K:w31:2:s P:w31
+K:w31:3:s M:21 S:21 I:21 Q:w30 Q:w31 H:w31 R:21 A:20 P:w40 K:w40:0:s P:w40 K:w40:1:s M:22 S:22 I:22 R:22
+A:21 P:w40 K:w40:2:s P:w40 K:w40:3:s M:23 S:23 I:23 R:23 A:22 P:w41 K:w41:0:s P:w41 K:w41:1:v M:30 S:30
+I:30 R:30 A:23 P:w41 K:w41:2:s P:w41 K:w41:3:s M:31 S:31 I:31 Q:w40 Q:w41 H:w41 R:31 A:30 P:w50 K:w50:0:s
+P:w50 K:w50:1:s M:32 S:32 I:32 R:32 A:31 P:w50 K:w50:2:s P:w50 K:w50:3:s M:33 S:33 I:33 R:33 A:32 P:w51
+K:w51:0:s P:w51 K:w51:1:v M:40 S:40 I:40 R:40 A:33 P:w51 K:w51:2:s P:w51 K:w51:3:s M:41 S:41 I:41 Q:w50
+Q:w51 H:w51 R:41 A:40 M:42 S:42 I:42 R:42 A:41 M:43 S:43 I:43 M:50 C:0 R:43 A:42:v M:51 C:1 M:52 C:2
+A:43:v M:53 C:3
+"""
 
 
 def tile_attention_pa_kernel(tc, x, freqs_cis, wqkv, q_norm_w, k_norm_w, out_0, out_1, out_2):
     nc = tc.nc
-    K = KNOBS
-    W_BUFS = K['W_BUFS']
     with ExitStack() as ctx:
         const = ctx.enter_context(tc.tile_pool(name="const", bufs=1))
-        w_pool = ctx.enter_context(tc.tile_pool(name="w_pool", bufs=W_BUFS))
+        w_pool = ctx.enter_context(tc.tile_pool(name="w_pool", bufs=3))
         stage = ctx.enter_context(tc.tile_pool(name="stage", bufs=3))
-        quantised = ctx.enter_context(tc.tile_pool(name="quantised", bufs=K.get('q_bufs', 5)))
+        quantised = ctx.enter_context(tc.tile_pool(name="quantised", bufs=5))
         work = ctx.enter_context(tc.tile_pool(name="work", bufs=4))
-        results = ctx.enter_context(tc.tile_pool(name="results", bufs=K['res_bufs']))
+        results = ctx.enter_context(tc.tile_pool(name="results", bufs=8))
         small = ctx.enter_context(tc.tile_pool(name="small", bufs=4))
-        t_psum = ctx.enter_context(tc.psum_pool(name="t_psum", bufs=K.get('t_banks', 4)))
-        acc_psum = ctx.enter_context(tc.psum_pool(name="acc_psum", bufs=8 - K.get('t_banks', 4)))
+        t_psum = ctx.enter_context(tc.psum_pool(name="t_psum", bufs=4))
+        acc_psum = ctx.enter_context(tc.psum_pool(name="acc_psum", bufs=8 - 4))
         ctx.enter_context(tc.manual_schedule())
 
         x_rows_dram = x.rearrange("b s k -> (b s) k")
@@ -58,44 +75,40 @@ def tile_attention_pa_kernel(tc, x, freqs_cis, wqkv, q_norm_w, k_norm_w, out_0, 
         ]
 
         gain_row = const.tile([P, 2, HD], BF16, name="gain_row")
-        nc.vector.memset(gain_row[:], 0.0)
         freqs = const.tile([P, 2, HP, 2], BF16, name="freqs")
         x_rows = const.tile([P, TOKEN_TILES, D], BF16, name="x_rows")
-
-        def load_x(m):
-            n = K.get('x_split', 1) if m == 0 else 1
-            w = D // n
-            for i in range(n):
-                nc.sync.dma_start(out=x_rows[:, m, w * i : w * (i + 1)], in_=x_rows_dram[P * m : P * (m + 1), w * i : w * (i + 1)])
-
+        eps = const.tile([P, 1], F32, name="eps")
+        warm = const.tile([P, 1], F32, name="warm")
+        ones = const.tile([P, P], BF16, name="ones")
+        wide_ones = const.tile([P, GROUP], BF16, name="wide_ones")
+        ident = const.tile([P, P], F32, name="ident")
+        gains = const.tile([P, 2, HP, 2], F32, name="gains")
         w_rows = {}
 
-        def load_w(g):
+        def load_x(m):
+            nc.sync.dma_start(out=x_rows[:, m, :], in_=x_rows_dram[P * m : P * (m + 1), :])
+
+        def load_w(g, how):
             w_rows[g] = w_pool.tile([P, HEADS, D], BF16, name="w_rows")
-            n = K.get('w0_split', 1) if g == 0 else 1
-            w = D // n
-            for b in range(2):
-                first = GROUP * g + HALF * b
-                for i in range(n):
+            per, parts = {"h": (1, 1), "q": (2, 2), "b": (2, 1), "p": (4, 2)}[how]
+            for b in range(HEADS // per):
+                first = GROUP * g + P * per * b
+                w = D // parts
+                for i in range(parts):
                     nc.sync.dma_start(
-                        out=w_rows[g][:, 2 * b : 2 * b + 2, w * i : w * (i + 1)],
-                        in_=wqkv[first : first + HALF, w * i : w * (i + 1)].rearrange("(h p) k -> p h k", p=P),
+                        out=w_rows[g][:, per * b : per * (b + 1), w * i : w * (i + 1)],
+                        in_=wqkv[first : first + P * per, w * i : w * (i + 1)].rearrange("(h p) k -> p h k", p=P),
                     )
 
-        def load_small():
-            nc.sync.dma_start(out=gain_row[0:1, 0, :], in_=q_norm_w.unsqueeze(0))
-            nc.sync.dma_start(out=gain_row[0:1, 1, :], in_=k_norm_w.unsqueeze(0))
-            nc.sync.dma_start(out=freqs[:], in_=freqs_cis.rearrange("(a p) j t -> p a j t", p=P))
+        def load_head(h):
+            if 0 not in w_rows:
+                w_rows[0] = w_pool.tile([P, HEADS, D], BF16, name="w_rows")
+            nc.sync.dma_start(out=w_rows[0][:, h, :], in_=wqkv[P * h : P * (h + 1), :])
 
-        eps = const.tile([P, 1], F32, name="eps")
-        nc.vector.memset(eps[:], EPS)
-        warm = const.tile([P, 1], F32, name="warm")
-        nc.scalar.activation(out=warm[:], in_=eps[:], func=ACT.Abs_reciprocal_sqrt)
-        ones = const.tile([P, P], BF16, name="ones")
-        nc.vector.memset(ones[:], 1.0)
-        ident = const.tile([P, P], F32, name="ident")
-        make_identity(nc, ident[:])
-        gains = const.tile([P, 2, HP, 2], F32, name="gains")
+        def load_small(queue):
+            queue.dma_start(out=gain_row[0:1, 0, :], in_=q_norm_w.unsqueeze(0))
+            queue.dma_start(out=gain_row[0:1, 1, :], in_=k_norm_w.unsqueeze(0))
+            queue.dma_start(out=freqs[:], in_=freqs_cis.rearrange("(a p) j t -> p a j t", p=P))
 
         def spread_gains():
             gain_bank = t_psum.tile([P, 2, HALF], F32, name="bank")
@@ -127,124 +140,194 @@ def tile_attention_pa_kernel(tc, x, freqs_cis, wqkv, q_norm_w, k_norm_w, out_0, 
             )
             factors[(kind, a)] = table
 
+        dummy_bank = {}
+
+        def dummy(n):
+            if 0 not in dummy_bank:
+                dummy_bank[0] = acc_psum.tile([P, HEADS, HD], F32, name="acc")
+            flat = dummy_bank[0][:].rearrange("p h d -> p (h d)")
+            nc.tensor.matmul(out=flat[:, 0:n], lhsT=ones[:], rhs=wide_ones[:, 0:n], start=True, stop=True)
+
+        x_codes = const.tile([P, TOKEN_TILES, PASSES * P], U32, align_bytes=64, name="x_codes")
+        x_scales = const.tile([P, TOKEN_TILES, PASSES * P], U8, align_bytes=64, name="x_scales")
+        operand = {}
         units = {}
 
-        def new_unit(key, pieces, codes, scales):
+        def new_unit(name):
+            kind = name[0]
+            if kind == "x":
+                m = int(name[1])
+                pieces = [(x_rows[:, m, :], c) for c in range(PASSES)]
+                codes, scales = x_codes[:, m, :], x_scales[:, m, :]
+            elif kind == "w":
+                g, half = int(name[1]), int(name[2])
+                ct = quantised.tile([P, 2, GROUP], U32, align_bytes=64, name="w_codes")
+                st = quantised.tile([P, 2, GROUP], U8, align_bytes=64, name="w_scales")
+                operand[name] = (ct, st)
+                pieces = [(w_rows[g][:, h, :], 2 * half + i) for i in range(2) for h in range(HEADS)]
+                codes, scales = ct[:].rearrange("p c n -> p (c n)"), st[:].rearrange("p c n -> p (c n)")
+            elif kind == "h":
+                b = int(name[1])
+                ct = quantised.tile([P, PASSES, HALF], U32, align_bytes=64, name="w_codes")
+                st = quantised.tile([P, PASSES, HALF], U8, align_bytes=64, name="w_scales")
+                operand[name] = (ct, st)
+                pieces = [(w_rows[0][:, 2 * b + i, :], c) for c in range(PASSES) for i in range(2)]
+                codes, scales = ct[:].rearrange("p c n -> p (c n)"), st[:].rearrange("p c n -> p (c n)")
+            elif kind == "k":
+                h = int(name[1])
+                ct = const.tile([P, PASSES, HD], U32, align_bytes=64, name="k_codes%d" % h)
+                st = const.tile([P, PASSES, HD], U8, align_bytes=64, name="k_scales%d" % h)
+                operand[name] = (ct, st)
+                pieces = [(w_rows[0][:, h, :], c) for c in range(PASSES)]
+                codes, scales = ct[:].rearrange("p c n -> p (c n)"), st[:].rearrange("p c n -> p (c n)")
+            else:
+                c, b = int(name[1]), int(name[2])
+                whole = "w0%d" % (c // 2)
+                if whole not in operand:
+                    operand[whole] = (
+                        quantised.tile([P, 2, GROUP], U32, align_bytes=64, name="w_codes"),
+                        quantised.tile([P, 2, GROUP], U8, align_bytes=64, name="w_scales"),
+                    )
+                ct, st = operand[whole]
+                pieces = [(w_rows[0][:, 2 * b + i, :], c) for i in range(2)]
+                codes = ct[:, c % 2, HALF * b : HALF * (b + 1)]
+                scales = st[:, c % 2, HALF * b : HALF * (b + 1)]
             banks = len(pieces) // 2
             grouped = stage.tile([P, banks * HALF, PACK], BF16, align_bytes=64, name="grouped%d" % banks)
-            units[key] = dict(pieces=pieces, codes=codes, scales=scales, grouped=grouped, banks={})
+            units[name] = [pieces, codes, scales, grouped, []]
 
-        def unit_T(key, n):
-            u = units[key]
+        def turn_bank(name):
+            if name not in units:
+                new_unit(name)
+            unit = units[name]
+            n = len(unit[4])
             bank = t_psum.tile([P, 2, HALF], F32, name="bank")
-            u['banks'][n] = bank
-            for uu in range(2):
+            unit[4].append(bank)
+            for u in range(2):
                 for i in range(2):
-                    rows, c = u['pieces'][2 * n + i]
-                    first = WORDS_PASS * c + P * uu
+                    rows, c = unit[0][2 * n + i]
+                    first = WORDS_PASS * c + P * u
                     nc.tensor.transpose(
-                        out=bank[:, uu, P * i : P * (i + 1)], in_=rows.bitcast(F32)[:, first : first + P], identity=ident[:]
+                        out=bank[:, u, P * i : P * (i + 1)],
+                        in_=rows.bitcast(F32)[:, first : first + P],
+                        identity=ident[:],
                     )
+            return n
 
-        def unit_C(key, n, on_vector):
-            u = units[key]
-            dst = u['grouped'][:].bitcast(F32)[:, HALF * n : HALF * (n + 1), :]
-            src = u['banks'][n][:].rearrange("p u n -> p n u")
+        def copy_bank(name, n, on_vector):
+            unit = units[name]
+            dst = unit[3][:].bitcast(F32)[:, HALF * n : HALF * (n + 1), :]
+            src = unit[4][n][:].rearrange("p u n -> p n u")
             if on_vector:
                 nc.vector.tensor_copy(out=dst, in_=src)
             else:
                 nc.scalar.copy(out=dst, in_=src)
 
-        def unit_Q(key):
-            u = units[key]
-            nc.vector.quantize_mx(
-                out=u['codes'].bitcast(FP8X4), scales=u['scales'], in_=u['grouped'][:].rearrange("p n t -> p (n t)")
-            )
+        def turn(name, spec):
+            for letter in spec:
+                n = turn_bank(name)
+                if letter in "SV":
+                    dummy(DUMMY)
+                copy_bank(name, n, letter in "vV")
 
-        def unit_H(key):
+        def quantise(name):
+            pieces, codes, scales, grouped, banks = units[name]
+            nc.vector.quantize_mx(out=codes.bitcast(FP8X4), scales=scales, in_=grouped[:].rearrange("p n t -> p (n t)"))
+
+        def hold(name):
             held = small.tile([P, 1], U32, name="held")
-            nc.gpsimd.tensor_copy(out=held[:], in_=units[key]['codes'][:, 0:1])
-
-        x_codes = const.tile([P, TOKEN_TILES, PASSES * P], U32, align_bytes=64, name="x_codes")
-        x_scales = const.tile([P, TOKEN_TILES, PASSES * P], U8, align_bytes=64, name="x_scales")
-        w_operand = {}
-
-        def new_w_half(g, half):
-            codes = quantised.tile([P, 2, GROUP], U32, align_bytes=64, name="w_codes")
-            scales = quantised.tile([P, 2, GROUP], U8, align_bytes=64, name="w_scales")
-            w_operand[(g, half)] = (codes, scales)
-
-        def make_x_unit(m):
-            new_unit(('x', m), [(x_rows[:, m, :], c) for c in range(PASSES)], x_codes[:, m, :], x_scales[:, m, :])
-
-        def make_w_unit(g, half):
-            new_w_half(g, half)
-            codes, scales = w_operand[(g, half)]
-            new_unit(
-                ('w', g, half),
-                [(w_rows[g][:, h, :], 2 * half + i) for i in range(2) for h in range(HEADS)],
-                codes[:].rearrange("p c n -> p (c n)"),
-                scales[:].rearrange("p c n -> p (c n)"),
-            )
-
-        def make_w0_unit(c, b):
-            codes, scales = w_operand[(0, c // 2)]
-            new_unit(
-                ('w0', c, b),
-                [(w_rows[0][:, 2 * b + i, :], c) for i in range(2)],
-                codes[:, c % 2, HALF * b : HALF * (b + 1)],
-                scales[:, c % 2, HALF * b : HALF * (b + 1)],
-            )
-
-        def make_w0_half_unit(b):
-            codes = quantised.tile([P, PASSES, HALF], U32, align_bytes=64, name="w_codes")
-            scales = quantised.tile([P, PASSES, HALF], U8, align_bytes=64, name="w_scales")
-            w_operand[('h', b)] = (codes, scales)
-            new_unit(
-                ('w0h', b),
-                [(w_rows[0][:, 2 * b + i, :], c) for c in range(PASSES) for i in range(2)],
-                codes[:].rearrange("p c n -> p (c n)"),
-                scales[:].rearrange("p c n -> p (c n)"),
-            )
+            nc.gpsimd.tensor_copy(out=held[:], in_=units[name][1][:, 0:1])
 
         accs = {}
+        sums = {}
         invs = {}
         prods = {}
-        pair_tiles = {}
 
-        def MM(g, m):
-            if g == V_GROUP and K.get('v_in_t', True):
-                acc = t_psum.tile([P, 2, HALF], F32, name="bank")
-                flat = acc[:].rearrange("p u n -> p (u n)")
-            else:
-                acc = acc_psum.tile([P, HEADS, HD], F32, name="acc")
-                flat = acc[:].rearrange("p h d -> p (h d)")
-            accs[(g, m)] = (acc, flat)
-            if g == 0 and K.get('w0_halves'):
-                for b in range(2):
-                    codes, scales = w_operand[('h', b)]
-                    for c in range(PASSES):
-                        nc.tensor.matmul_mx(
-                            out=flat[:, HALF * b : HALF * (b + 1)],
-                            lhsT=x_codes[:, m, P * c : P * (c + 1)].bitcast(FP8X4),
-                            lhsT_scale=x_scales[:, m, P * c : P * (c + 1)],
-                            rhs=codes[:, c, :].bitcast(FP8X4),
-                            rhs_scale=scales[:, c, :],
-                            start=(c == 0),
-                            stop=(c == PASSES - 1),
-                        )
-                return
+        def product_half(m, b):
+            acc = t_psum.tile([P, 2, HALF], F32, name="bank")
+            accs[(V_GROUP, m, b)] = acc
             for c in range(PASSES):
-                codes, scales = w_operand[(g, c // 2)]
+                codes, scales = operand["w%d%d" % (V_GROUP, c // 2)]
                 nc.tensor.matmul_mx(
-                    out=flat,
+                    out=acc[:, 0, :],
                     lhsT=x_codes[:, m, P * c : P * (c + 1)].bitcast(FP8X4),
                     lhsT_scale=x_scales[:, m, P * c : P * (c + 1)],
-                    rhs=codes[:, c % 2, :].bitcast(FP8X4),
-                    rhs_scale=scales[:, c % 2, :],
+                    rhs=codes[:, c % 2, HALF * b : HALF * (b + 1)].bitcast(FP8X4),
+                    rhs_scale=scales[:, c % 2, HALF * b : HALF * (b + 1)],
                     start=(c == 0),
                     stop=(c == PASSES - 1),
                 )
+
+        def copy_half(m, b, engine_copy):
+            half_result = results.tile([P, HALF], F32, name="half_result")
+            engine_copy(out=half_result[:], in_=accs[(V_GROUP, m, b)][:, 0, :])
+            nc.sync.dma_start(out=out_dram[2][P * m : P * (m + 1), HALF * b : HALF * (b + 1)], in_=half_result[:])
+
+        def product(g, m, part):
+            if (g, m) not in accs:
+                if g == V_GROUP:
+                    acc = t_psum.tile([P, 2, HALF], F32, name="bank")
+                    accs[(g, m)] = (acc, acc[:].rearrange("p u n -> p (u n)"))
+                else:
+                    acc = acc_psum.tile([P, HEADS, HD], F32, name="acc")
+                    accs[(g, m)] = (acc, acc[:].rearrange("p h d -> p (h d)"))
+            flat = accs[(g, m)][1]
+            passes = {"a": (0, 1), "b": (2, 3)}.get(part, range(PASSES))
+            part = "" if part in ("a", "b") else part
+            for c in passes:
+                if part:
+                    codes, scales = operand[part]
+                    width = HALF if part[0] == "h" else HD
+                    at = width * int(part[1])
+                    rhs, rhs_scale = codes[:, c, :], scales[:, c, :]
+                else:
+                    codes, scales = operand["w%d%d" % (g, c // 2)]
+                    at, width = 0, GROUP
+                    rhs, rhs_scale = codes[:, c % 2, :], scales[:, c % 2, :]
+                nc.tensor.matmul_mx(
+                    out=flat[:, at : at + width],
+                    lhsT=x_codes[:, m, P * c : P * (c + 1)].bitcast(FP8X4),
+                    lhsT_scale=x_scales[:, m, P * c : P * (c + 1)],
+                    rhs=rhs.bitcast(FP8X4),
+                    rhs_scale=rhs_scale,
+                    start=(c == 0),
+                    stop=(c == PASSES - 1),
+                )
+
+        def squares_of(g, m, heads):
+            acc = accs[(g, m)][0]
+            if (g, m) not in sums:
+                sums[(g, m)] = small.tile([P, HEADS], F32, name="sumsq")
+            sumsq = sums[(g, m)]
+            for h in heads:
+                squares = small.tile([P, HD], BF16, name="squares")
+                nc.scalar.activation(out=squares[:], in_=acc[:, h, :], func=ACT.Square, accum_out=sumsq[:, h : h + 1])
+
+        def inverse(g, m):
+            inv = small.tile([P, HEADS], F32, name="inv")
+            nc.scalar.activation(
+                out=inv[:], in_=sums[(g, m)][:], func=ACT.Abs_reciprocal_sqrt, bias=eps[:, 0:1], scale=1.0 / HD
+            )
+            invs[(g, m)] = inv
+
+        def rotate(g, m, heads):
+            acc = accs[(g, m)][0]
+            inv = invs[(g, m)]
+            table = factors[(0 if g < Q_GROUPS else 1, m % 2)]
+            if (g, m) not in prods:
+                prods[(g, m)] = work.tile([P, 2, HEADS * HP, 2], F32, name="products")
+            products = prods[(g, m)]
+            for h in heads:
+                nc.vector.scalar_tensor_tensor(
+                    out=products[:, :, HP * h : HP * (h + 1), :].rearrange("p k j e -> p k (j e)"),
+                    in0=acc[:, h, :].unsqueeze(1).to_broadcast([P, 2, HD]),
+                    scalar=inv[:, h : h + 1],
+                    in1=table[:].rearrange("p k j e -> p k (j e)"),
+                    op0=ALU.mult,
+                    op1=ALU.mult,
+                )
+
+        pending = {}
 
         def store(g, m, result):
             if g < Q_GROUPS:
@@ -255,321 +338,83 @@ def tile_attention_pa_kernel(tc, x, freqs_cis, wqkv, q_norm_w, k_norm_w, out_0, 
                 dst = out_dram[2][P * m : P * (m + 1), :]
             nc.sync.dma_start(out=dst, in_=result)
 
-        def SQ(g, m):
-            acc = accs[(g, m)][0]
-            sumsq = small.tile([P, HEADS], F32, name="sumsq")
-            for h in range(HEADS):
-                squares = small.tile([P, HD], BF16, name="squares")
-                nc.scalar.activation(out=squares[:], in_=acc[:, h, :], func=ACT.Square, accum_out=sumsq[:, h : h + 1])
-            inv = small.tile([P, HEADS], F32, name="inv")
-            nc.scalar.activation(out=inv[:], in_=sumsq[:], func=ACT.Abs_reciprocal_sqrt, bias=eps[:, 0:1], scale=1.0 / HD)
-            invs[(g, m)] = inv
-
-        def STT(g, m):
-            acc = accs[(g, m)][0]
-            inv = invs[(g, m)]
-            table = factors[(0 if g < Q_GROUPS else 1, m % 2)]
-            if K.get('pairs'):
-                bank_no = TOKEN_TILES * g + m + K.get('pair_shift', 0)
-                if bank_no // 2 not in pair_tiles:
-                    pair_tiles[bank_no // 2] = (work.tile([P, 2, 2, HEADS * HP, 2], F32, name="products2"), [])
-                pair_tiles[bank_no // 2][1].append((bank_no % 2, g, m))
-                products = pair_tiles[bank_no // 2][0][:, bank_no % 2, :, :, :]
-            else:
-                products = work.tile([P, 2, HEADS * HP, 2], F32, name="products")
-            for h in range(HEADS):
-                nc.vector.scalar_tensor_tensor(
-                    out=products[:, :, HP * h : HP * (h + 1), :].rearrange("p k j e -> p k (j e)"),
-                    in0=acc[:, h, :].unsqueeze(1).to_broadcast([P, 2, HD]),
-                    scalar=inv[:, h : h + 1],
-                    in1=table[:].rearrange("p k j e -> p k (j e)"),
-                    op0=ALU.mult,
-                    op1=ALU.mult,
-                )
-            prods[(g, m)] = products
-
-        def ADD(g, m, on_vector=False):
+        def add(g, m, engine, later):
             products = prods[(g, m)]
             result = results.tile([P, HEADS * HP, 2], F32, name="result")
-            eng = nc.vector if on_vector else nc.gpsimd
-            eng.tensor_tensor(out=result[:], in0=products[:, 0, :, :], in1=products[:, 1, :, ::-1], op=ALU.add)
-            store(g, m, result[:].rearrange("p n e -> p (n e)"))
+            engine.tensor_tensor(out=result[:], in0=products[:, 0, :, :], in1=products[:, 1, :, ::-1], op=ALU.add)
+            if later:
+                pending[(g, m)] = result[:].rearrange("p n e -> p (n e)")
+            else:
+                store(g, m, result[:].rearrange("p n e -> p (n e)"))
 
-        def ADD2(g, pair, on_vector=False):
-            prod, members = pair_tiles[(TOKEN_TILES * g + pair + K.get('pair_shift', 0)) // 2]
-            result = results.tile([P, 2, HEADS * HP, 2], F32, name="result2")
-            eng = nc.vector if on_vector else nc.gpsimd
-            lo = min(member[0] for member in members)
-            hi = max(member[0] for member in members) + 1
-            eng.tensor_tensor(
-                out=result[:, lo:hi, :, :], in0=prod[:, lo:hi, 0, :, :], in1=prod[:, lo:hi, 1, :, ::-1], op=ALU.add
-            )
-            for s, gg, mm in members:
-                store(gg, mm, result[:, s, :, :].rearrange("p n e -> p (n e)"))
-
-        def VC(m):
-            flat = accs[(V_GROUP, m)][1]
+        def copy_v(m, engine_copy, later):
             v_result = results.tile([P, GROUP], F32, name="result")
-            nc.scalar.copy(out=v_result[:], in_=flat)
-            store(V_GROUP, m, v_result[:])
+            engine_copy(out=v_result[:], in_=accs[(V_GROUP, m)][1])
+            if later:
+                pending[(V_GROUP, m)] = v_result[:]
+            else:
+                store(V_GROUP, m, v_result[:])
 
-        ORDER(K, dict(load_x=load_x, load_w=load_w, load_small=load_small, spread_gains=spread_gains,
-                      make_factors=make_factors, make_x_unit=make_x_unit, make_w_unit=make_w_unit,
-                      make_w0_unit=make_w0_unit, make_w0_half_unit=make_w0_half_unit, new_w_half=new_w_half, T=unit_T, C=unit_C, Q=unit_Q, H=unit_H,
-                      MM=MM, SQ=SQ, STT=STT, ADD=ADD, ADD2=ADD2, VC=VC))
+        nc.vector.memset(gain_row[:], 0.0)
+        nc.vector.memset(eps[:], EPS)
+        nc.vector.memset(ones[:], 1.0)
+        nc.vector.memset(wide_ones[:], 1.0)
+        make_identity(nc, ident[:])
 
+        def warm_table():
+            nc.scalar.activation(out=warm[:], in_=eps[:], func=ACT.Abs_reciprocal_sqrt)
 
-def ORDER(K, f):
-    W_BUFS = K['W_BUFS']
-    f['load_x'](0)
-    if K.get('small_first'):
-        f['load_small']()
-    f['load_w'](0)
-    if not K.get('small_first'):
-        f['load_small']()
-    if K.get('w1_early'):
-        f['load_x'](1)
-        f['load_w'](1)
-        f['load_x'](2)
-        f['load_x'](3)
-        for g in range(2, W_BUFS):
-            f['load_w'](g)
-    else:
-        for m in range(1, TOKEN_TILES):
-            f['load_x'](m)
-        for g in range(1, W_BUFS):
-            f['load_w'](g)
-    if K['variant'] == 'A':
-        order_A(K, f)
-    elif K['variant'] == 'B':
-        order_B(K, f)
-    else:
-        order_C(K, f)
+        if "LS:a" not in PROGRAM:
+            warm_table()
 
-
-def whole_unit(f, key, banks, vset=()):
-    for n in range(banks):
-        f['T'](key, n)
-        f['C'](key, n, n in vset)
-    f['Q'](key)
-
-
-def order_A(K, f):
-    W_BUFS = K['W_BUFS']
-    f['new_w_half'](0, 0)
-    f['new_w_half'](0, 1)
-    f['make_x_unit'](0)
-    whole_unit(f, ('x', 0), 2, K.get('hx', ()))
-    for b in range(2):
-        for c in range(PASSES):
-            f['make_w0_unit'](c, b)
-            whole_unit(f, ('w0', c, b), 1, (0,) if (b, c) in K['head_v'] else ())
-    f['spread_gains']()
-    for m in range(1, TOKEN_TILES):
-        f['make_x_unit'](m)
-        whole_unit(f, ('x', m), 2, K.get('hx', ()))
-    for kind in range(2):
-        for a in range(2):
-            f['make_factors'](kind, a)
-    if W_BUFS < N_GROUPS:
-        f['load_w'](W_BUFS)
-    waiting = []
-    for m in range(TOKEN_TILES):
-        f['MM'](0, m)
-        f['SQ'](0, m)
-        if m == TOKEN_TILES - 1:
-            for half in range(2):
-                f['make_w_unit'](1, half)
-                whole_unit(f, ('w', 1, half), 4, K['vshare'][half])
-        f['STT'](0, m)
-        waiting.append((0, m))
-        if len(waiting) > 1:
-            f['ADD'](*waiting[-2])
-    for g in range(1, V_GROUP):
-        if W_BUFS <= g + W_BUFS < N_GROUPS:
-            f['load_w'](g + W_BUFS)
-        for m in range(TOKEN_TILES):
-            if m < 2:
-                f['make_w_unit'](g + 1, m)
-                whole_unit(f, ('w', g + 1, m), 4, K['vshare'][m])
-            f['MM'](g, m)
-            f['SQ'](g, m)
-            f['STT'](g, m)
-            waiting.append((g, m))
-            f['ADD'](*waiting[-2])
-            if g == K_GROUP and m >= 2:
-                for v_tile in range(2 * (m - 2), 2 * (m - 2) + 2):
-                    f['MM'](V_GROUP, v_tile)
-                    f['VC'](v_tile)
-    f['ADD'](*waiting[-1], on_vector=bool(K['last_add_v']))
-
-
-def order_B(K, f):
-    W_BUFS = K['W_BUFS']
-    f['new_w_half'](0, 0)
-    f['new_w_half'](0, 1)
-    f['make_x_unit'](0)
-    whole_unit(f, ('x', 0), 2, K.get('hx0', ()))
-
-    def tables():
-        f['spread_gains']()
-        for kind in range(2):
-            for a in range(2):
-                f['make_factors'](kind, a)
-
-    if K.get('small_first'):
-        tables()
-    for b in range(2):
-        for c in range(PASSES):
-            f['make_w0_unit'](c, b)
-            whole_unit(f, ('w0', c, b), 1, (0,) if (b, c) in K['head_v'] else ())
-    if not K.get('small_first'):
-        tables()
-    if W_BUFS < N_GROUPS:
-        f['load_w'](W_BUFS)
-    waiting = []
-    xa = K.get('x_ahead', 1)
-    for m in range(1, 1 + xa):
-        f['make_x_unit'](m)
-        whole_unit(f, ('x', m), 2, K.get('hx', ()))
-    for m in range(TOKEN_TILES):
-        f['MM'](0, m)
-        if m + 1 + xa < TOKEN_TILES + 1 and m + xa + 1 <= TOKEN_TILES - 1:
-            f['make_x_unit'](m + xa + 1)
-            whole_unit(f, ('x', m + xa + 1), 2, K.get('hx', ()))
-        f['SQ'](0, m)
-        if m == K.get('w1_at', TOKEN_TILES - 1):
-            for half in range(2):
-                f['make_w_unit'](1, half)
-                whole_unit(f, ('w', 1, half), 4, K.get('vshare1', K['vshare'])[half])
-        f['STT'](0, m)
-        waiting.append((0, m))
-        if len(waiting) > 1:
-            f['ADD'](*waiting[-2])
-    for g in range(1, V_GROUP):
-        if W_BUFS <= g + W_BUFS < N_GROUPS:
-            f['load_w'](g + W_BUFS)
-        for m in range(TOKEN_TILES):
-            if m < 2:
-                f['make_w_unit'](g + 1, m)
-                whole_unit(f, ('w', g + 1, m), 4, K['vshare'][m])
-            f['MM'](g, m)
-            f['SQ'](g, m)
-            f['STT'](g, m)
-            waiting.append((g, m))
-            f['ADD'](*waiting[-2])
-            if g == K_GROUP and not K.get('v_last') and m >= 2:
-                for v_tile in range(2 * (m - 2), 2 * (m - 2) + 2):
-                    f['MM'](V_GROUP, v_tile)
-                    f['VC'](v_tile)
-    if K.get('v_last'):
-        f['ADD'](*waiting[-1], on_vector=bool(K['last_add_v']))
-        for v_tile in range(TOKEN_TILES):
-            f['MM'](V_GROUP, v_tile)
-            f['VC'](v_tile)
-    else:
-        f['ADD'](*waiting[-1], on_vector=bool(K['last_add_v']))
-
-
-def run_seq(K, f, g, seq, prev):
-    for tok in seq.split():
-        if tok in ('UA', 'UB'):
-            half = 0 if tok == 'UA' else 1
-            if g + 1 > V_GROUP: continue
-            f['make_w_unit'](g + 1, half)
-            for n in range(4):
-                f['T'](('w', g + 1, half), n)
-                f['C'](('w', g + 1, half), n, n in K.get('vshare_g', {}).get(g + 1, K['vshare'])[half])
-        elif tok in ('UAa', 'UAb', 'UBa', 'UBb'):
-            half = 0 if tok[1] == 'A' else 1
-            if g + 1 > V_GROUP: continue
-            if tok[2] == 'a':
-                f['make_w_unit'](g + 1, half)
-            for n in ((0, 1) if tok[2] == 'a' else (2, 3)):
-                f['T'](('w', g + 1, half), n)
-                f['C'](('w', g + 1, half), n, n in K.get('vshare_g', {}).get(g + 1, K['vshare'])[half])
-        elif tok in ('NAa', 'NAb'):
-            if g + 2 > V_GROUP: continue
-            if tok[2] == 'a':
-                f['make_w_unit'](g + 2, 0)
-            for n in ((0, 1) if tok[2] == 'a' else (2, 3)):
-                f['T'](('w', g + 2, 0), n)
-                f['C'](('w', g + 2, 0), n, n in K.get('vshare_n', ()))
-        elif tok in ('QA', 'QB'):
-            if g + 1 > V_GROUP: continue
-            f['Q'](('w', g + 1, 0 if tok == 'QA' else 1))
-        elif tok in ('HA', 'HB'):
-            if g + 1 > V_GROUP: continue
-            f['H'](('w', g + 1, 0 if tok == 'HA' else 1))
-        elif tok.startswith('MM'):
-            f['MM'](g, int(tok[2:]))
-        elif tok.startswith('SQ'):
-            f['SQ'](g, int(tok[2:]))
-        elif tok.startswith('STT'):
-            f['STT'](g, int(tok[3:]))
-        elif tok.startswith('ADDW'):
-            f['ADD2'](g, int(tok[4]), on_vector=tok[-1] == 'v')
-        elif tok.startswith('ADDp'):
-            if prev is not None: f['ADD'](*prev, on_vector=tok[-1] == 'v')
-        elif tok.startswith('ADD'):
-            f['ADD'](g, int(tok[3]), on_vector=tok[-1] == 'v')
-        elif tok.startswith('VM'):
-            f['MM'](V_GROUP, int(tok[2:]))
-        elif tok.startswith('VC'):
-            f['VC'](int(tok[2:]))
-        elif tok.startswith('X'):
-            m = int(tok[1:])
-            f['make_x_unit'](m)
-            whole_unit(f, ('x', m), 2, K.get('hx', ()))
-        else:
-            raise ValueError(tok)
-
-
-SEQ06 = "UA QA HA MM0 SQ0 STT0 ADDp UB QB HB MM1 SQ1 STT1 ADD0 MM2 SQ2 STT2 ADD1 MM3 SQ3 STT3 ADD2"
-SEQ0 = "MM0 SQ0 STT0 MM1 SQ1 STT1 ADD0 MM2 SQ2 STT2 ADD1 MM3 SQ3 UA QA HA UB QB HB STT3 ADD2"
-SEQK = "MM0 SQ0 STT0 ADDp MM1 SQ1 STT1 ADD0 MM2 SQ2 STT2 ADD1 VM0 VC0 VM1 VC1 MM3 SQ3 STT3 ADD2 VM2 VC2 VM3 VC3 ADD3"
-
-
-def order_C(K, f):
-    W_BUFS = K['W_BUFS']
-    if not K.get('w0_halves'):
-        f['new_w_half'](0, 0)
-        f['new_w_half'](0, 1)
-    f['make_x_unit'](0)
-    whole_unit(f, ('x', 0), 2, K.get('hx0', ()))
-
-    def tables():
-        f['spread_gains']()
-        for kind in range(2):
-            for a in range(2):
-                f['make_factors'](kind, a)
-
-    if K.get('small_first'):
-        tables()
-    for b in range(2):
-        if K.get('w0_halves'):
-            f['make_w0_half_unit'](b)
-            whole_unit(f, ('w0h', b), 4, K.get('w0h_v', ()))
-            continue
-        for c in range(PASSES):
-            f['make_w0_unit'](c, b)
-            whole_unit(f, ('w0', c, b), 1, (0,) if (b, c) in K['head_v'] else ())
-    if not K.get('small_first') and not K.get('tables_late'):
-        f['spread_gains']()
-    run_seq(K, f, 0, K.get('seqx', 'X1 X2 X3'), None)
-    if not K.get('small_first'):
-        if K.get('tables_late'):
-            f['spread_gains']()
-        for kind in range(2):
-            for a in range(2):
-                f['make_factors'](kind, a)
-    if W_BUFS < N_GROUPS:
-        f['load_w'](W_BUFS)
-    run_seq(K, f, 0, K.get('seq0', SEQ0), None)
-    for g in range(1, V_GROUP):
-        if W_BUFS <= g + W_BUFS < N_GROUPS:
-            f['load_w'](g + W_BUFS)
-        if g < K_GROUP:
-            run_seq(K, f, g, K.get('seq1', K.get('seq', SEQ06)) if g == 1 else K.get('seq', SEQ06), (g - 1, 3))
-        else:
-            run_seq(K, f, g, K.get('seqk', "UA QA HA " + SEQK.replace("MM1", "UB QB HB MM1")), (g - 1, 3))
+        for token in PROGRAM.split():
+            part = token.split(":")
+            op = part[0]
+            arg = part[1] if len(part) > 1 else ""
+            extra = part[2] if len(part) > 2 else ""
+            if op == "LX":
+                load_x(int(arg))
+            elif op == "LW":
+                load_w(int(arg), extra)
+            elif op == "LS":
+                load_small(nc.scalar if arg == "a" else nc.sync)
+                if arg == "a":
+                    warm_table()
+            elif op == "G":
+                spread_gains()
+            elif op == "F":
+                make_factors(int(arg[0]), int(arg[1]))
+            elif op == "D":
+                dummy(int(arg))
+            elif op == "T":
+                turn(arg, extra)
+            elif op == "P":
+                turn_bank(arg)
+            elif op == "K":
+                copy_bank(arg, int(extra), part[3] == "v")
+            elif op == "Q":
+                quantise(arg)
+            elif op == "H":
+                hold(arg)
+            elif op == "M":
+                product(int(arg[0]), int(arg[1]), extra)
+            elif op == "S":
+                squares_of(int(arg[0]), int(arg[1]), [int(h) for h in (extra or "0123")])
+            elif op == "I":
+                inverse(int(arg[0]), int(arg[1]))
+            elif op == "R":
+                rotate(int(arg[0]), int(arg[1]), [int(h) for h in (extra or "0123")])
+            elif op == "A":
+                add(int(arg[0]), int(arg[1]), nc.vector if "v" in extra else nc.gpsimd, "l" in extra)
+            elif op == "C":
+                copy_v(int(arg), nc.vector.tensor_copy if "v" in extra else nc.scalar.copy, "l" in extra)
+            elif op == "MH":
+                product_half(int(arg[0]), int(arg[1]))
+            elif op == "CH":
+                copy_half(int(arg[0]), int(arg[1]), nc.vector.tensor_copy if "v" in extra else nc.scalar.copy)
+            elif op == "LH":
+                load_head(int(arg))
+            elif op == "O":
+                store(int(arg[0]), int(arg[1]), pending[(int(arg[0]), int(arg[1]))])
+            else:
+                raise ValueError(token)

@@ -30,7 +30,6 @@ V_GROUP = 5
 N_GROUPS = 6
 EPS = 1e-6
 FLOPS = 2 * TOKENS * D * (N_GROUPS * GROUP)
-DUMMY = 320
 
 PROGRAM = """
 LX:0 LW:0:q LS:s LX:1 LX:2 LX:3 LW:1:b LW:2:b P:x0 K:x0:0:s P:x0 K:x0:1:s Q:x0 P:u00 K:u00:0:s Q:u00
@@ -59,10 +58,12 @@ def tile_attention_pa_kernel(tc, x, freqs_cis, wqkv, q_norm_w, k_norm_w, out_0, 
         const = ctx.enter_context(tc.tile_pool(name="const", bufs=1))
         w_pool = ctx.enter_context(tc.tile_pool(name="w_pool", bufs=3))
         stage = ctx.enter_context(tc.tile_pool(name="stage", bufs=3))
+        head_stage = ctx.enter_context(tc.tile_pool(name="head_stage", bufs=2))
         quantised = ctx.enter_context(tc.tile_pool(name="quantised", bufs=5))
-        work = ctx.enter_context(tc.tile_pool(name="work", bufs=4))
-        results = ctx.enter_context(tc.tile_pool(name="results", bufs=8))
+        work = ctx.enter_context(tc.tile_pool(name="work", bufs=20))
+        results = ctx.enter_context(tc.tile_pool(name="results", bufs=4))
         small = ctx.enter_context(tc.tile_pool(name="small", bufs=4))
+        norms = ctx.enter_context(tc.tile_pool(name="norms", bufs=20))
         t_psum = ctx.enter_context(tc.psum_pool(name="t_psum", bufs=4))
         acc_psum = ctx.enter_context(tc.psum_pool(name="acc_psum", bufs=8 - 4))
         ctx.enter_context(tc.manual_schedule())
@@ -80,7 +81,6 @@ def tile_attention_pa_kernel(tc, x, freqs_cis, wqkv, q_norm_w, k_norm_w, out_0, 
         eps = const.tile([P, 1], F32, name="eps")
         warm = const.tile([P, 1], F32, name="warm")
         ones = const.tile([P, P], BF16, name="ones")
-        wide_ones = const.tile([P, GROUP], BF16, name="wide_ones")
         ident = const.tile([P, P], F32, name="ident")
         gains = const.tile([P, 2, HP, 2], F32, name="gains")
         w_rows = {}
@@ -140,14 +140,6 @@ def tile_attention_pa_kernel(tc, x, freqs_cis, wqkv, q_norm_w, k_norm_w, out_0, 
             )
             factors[(kind, a)] = table
 
-        dummy_bank = {}
-
-        def dummy(n):
-            if 0 not in dummy_bank:
-                dummy_bank[0] = acc_psum.tile([P, HEADS, HD], F32, name="acc")
-            flat = dummy_bank[0][:].rearrange("p h d -> p (h d)")
-            nc.tensor.matmul(out=flat[:, 0:n], lhsT=ones[:], rhs=wide_ones[:, 0:n], start=True, stop=True)
-
         x_codes = const.tile([P, TOKEN_TILES, PASSES * P], U32, align_bytes=64, name="x_codes")
         x_scales = const.tile([P, TOKEN_TILES, PASSES * P], U8, align_bytes=64, name="x_scales")
         operand = {}
@@ -193,7 +185,9 @@ def tile_attention_pa_kernel(tc, x, freqs_cis, wqkv, q_norm_w, k_norm_w, out_0, 
                 codes = ct[:, c % 2, HALF * b : HALF * (b + 1)]
                 scales = st[:, c % 2, HALF * b : HALF * (b + 1)]
             banks = len(pieces) // 2
-            grouped = stage.tile([P, banks * HALF, PACK], BF16, align_bytes=64, name="grouped%d" % banks)
+            grouped = (stage if banks == 4 else head_stage).tile(
+                [P, banks * HALF, PACK], BF16, align_bytes=64, name="grouped%d" % banks
+            )
             units[name] = [pieces, codes, scales, grouped, []]
 
         def turn_bank(name):
@@ -226,8 +220,6 @@ def tile_attention_pa_kernel(tc, x, freqs_cis, wqkv, q_norm_w, k_norm_w, out_0, 
         def turn(name, spec):
             for letter in spec:
                 n = turn_bank(name)
-                if letter in "SV":
-                    dummy(DUMMY)
                 copy_bank(name, n, letter in "vV")
 
         def quantise(name):
@@ -297,14 +289,14 @@ def tile_attention_pa_kernel(tc, x, freqs_cis, wqkv, q_norm_w, k_norm_w, out_0, 
         def squares_of(g, m, heads):
             acc = accs[(g, m)][0]
             if (g, m) not in sums:
-                sums[(g, m)] = small.tile([P, HEADS], F32, name="sumsq")
+                sums[(g, m)] = norms.tile([P, HEADS], F32, name="sumsq")
             sumsq = sums[(g, m)]
             for h in heads:
                 squares = small.tile([P, HD], BF16, name="squares")
                 nc.scalar.activation(out=squares[:], in_=acc[:, h, :], func=ACT.Square, accum_out=sumsq[:, h : h + 1])
 
         def inverse(g, m):
-            inv = small.tile([P, HEADS], F32, name="inv")
+            inv = norms.tile([P, HEADS], F32, name="inv")
             nc.scalar.activation(
                 out=inv[:], in_=sums[(g, m)][:], func=ACT.Abs_reciprocal_sqrt, bias=eps[:, 0:1], scale=1.0 / HD
             )
@@ -340,12 +332,12 @@ def tile_attention_pa_kernel(tc, x, freqs_cis, wqkv, q_norm_w, k_norm_w, out_0, 
 
         def add(g, m, engine, later):
             products = prods[(g, m)]
-            result = results.tile([P, HEADS * HP, 2], F32, name="result")
-            engine.tensor_tensor(out=result[:], in0=products[:, 0, :, :], in1=products[:, 1, :, ::-1], op=ALU.add)
+            result = products[:, 0, :, :]
+            engine.tensor_tensor(out=result, in0=result, in1=products[:, 1, :, ::-1], op=ALU.add)
             if later:
-                pending[(g, m)] = result[:].rearrange("p n e -> p (n e)")
+                pending[(g, m)] = result.rearrange("p n e -> p (n e)")
             else:
-                store(g, m, result[:].rearrange("p n e -> p (n e)"))
+                store(g, m, result.rearrange("p n e -> p (n e)"))
 
         def copy_v(m, engine_copy, later):
             v_result = results.tile([P, GROUP], F32, name="result")
@@ -358,7 +350,6 @@ def tile_attention_pa_kernel(tc, x, freqs_cis, wqkv, q_norm_w, k_norm_w, out_0, 
         nc.vector.memset(gain_row[:], 0.0)
         nc.vector.memset(eps[:], EPS)
         nc.vector.memset(ones[:], 1.0)
-        nc.vector.memset(wide_ones[:], 1.0)
         make_identity(nc, ident[:])
 
         def warm_table():
@@ -384,8 +375,6 @@ def tile_attention_pa_kernel(tc, x, freqs_cis, wqkv, q_norm_w, k_norm_w, out_0, 
                 spread_gains()
             elif op == "F":
                 make_factors(int(arg[0]), int(arg[1]))
-            elif op == "D":
-                dummy(int(arg))
             elif op == "T":
                 turn(arg, extra)
             elif op == "P":

@@ -58,9 +58,10 @@ def tile_attention_pa_kernel(tc, x, freqs_cis, wqkv, q_norm_w, k_norm_w, out_0, 
         const = ctx.enter_context(tc.tile_pool(name="const", bufs=1))
         w_pool = ctx.enter_context(tc.tile_pool(name="w_pool", bufs=3))
         stage = ctx.enter_context(tc.tile_pool(name="stage", bufs=3))
-        head_stage = ctx.enter_context(tc.tile_pool(name="head_stage", bufs=2))
+        x_stage = ctx.enter_context(tc.tile_pool(name="x_stage", bufs=3))
+        head_stage = ctx.enter_context(tc.tile_pool(name="head_stage", bufs=8))
         quantised = ctx.enter_context(tc.tile_pool(name="quantised", bufs=5))
-        work = ctx.enter_context(tc.tile_pool(name="work", bufs=20))
+        work = ctx.enter_context(tc.tile_pool(name="work", bufs=14))
         results = ctx.enter_context(tc.tile_pool(name="results", bufs=4))
         small = ctx.enter_context(tc.tile_pool(name="small", bufs=4))
         norms = ctx.enter_context(tc.tile_pool(name="norms", bufs=20))
@@ -185,7 +186,7 @@ def tile_attention_pa_kernel(tc, x, freqs_cis, wqkv, q_norm_w, k_norm_w, out_0, 
                 codes = ct[:, c % 2, HALF * b : HALF * (b + 1)]
                 scales = st[:, c % 2, HALF * b : HALF * (b + 1)]
             banks = len(pieces) // 2
-            grouped = (stage if banks == 4 else head_stage).tile(
+            grouped = {4: stage, 2: x_stage, 1: head_stage}[banks].tile(
                 [P, banks * HALF, PACK], BF16, align_bytes=64, name="grouped%d" % banks
             )
             units[name] = [pieces, codes, scales, grouped, []]

from contextlib import ExitStack

import concourse.mybir as mybir
from concourse.masks import make_identity

F32 = mybir.dt.float32
BF16 = mybir.dt.bfloat16
U32 = mybir.dt.uint32
U8 = mybir.dt.uint8
FP8X4 = mybir.dt.float8_e4m3fn_x4
ALU = mybir.AluOpType
ACT = mybir.ActivationFunctionType

P = 128
PACK = 4
K_PASS = P * PACK
WORDS_PASS = K_PASS // 2
TOKENS = 512
D = 2048
PASSES = D // K_PASS
TOKEN_TILES = TOKENS // P
HD = 128
HP = HD // 2
HEADS = 4
GROUP = HEADS * HD
HALF = GROUP // 2
Q_GROUPS = 4
K_GROUP = 4
V_GROUP = 5
N_GROUPS = 6
EPS = 1e-6
FLOPS = 2 * TOKENS * D * (N_GROUPS * GROUP)

PROGRAM = """
LX:0 LW:0:q LS:s LX:1 LX:2 LX:3 LW:1:b LW:2:b P:x0 K:x0:0:s P:x0 K:x0:1:s Q:x0 P:u00 K:u00:0:s Q:u00
P:u10 K:u10:0:s Q:u10 P:u20 K:u20:0:s Q:u20 P:u30 K:u30:0:s Q:u30 P:u01 K:u01:0:s Q:u01 P:u11 K:u11:0:s
Q:u11 P:u21 K:u21:0:s Q:u21 P:u31 K:u31:0:s Q:u31 G P:x1 K:x1:0:s P:x1 K:x1:1:s Q:x1 P:x2 K:x2:0:s P:x2
K:x2:1:s Q:x2 P:x3 K:x3:0:s P:x3 K:x3:1:s Q:x3 F:00 F:01 F:10 F:11 LW:3:b M:00 S:00 I:00 R:00 M:01 S:01
I:01 R:01 A:00 M:02 S:02 I:02 R:02 A:01 M:03 S:03 I:03 P:w10 K:w10:0:s P:w10 K:w10:1:s P:w10 K:w10:2:s
P:w10 K:w10:3:s P:w11 K:w11:0:s P:w11 K:w11:1:v P:w11 K:w11:2:s P:w11 K:w11:3:s Q:w10 Q:w11 H:w11 R:03
A:02 LW:4:b P:w20 K:w20:0:s P:w20 K:w20:1:s P:w20 K:w20:2:s P:w20 K:w20:3:s M:10 S:10 I:10 R:10 A:03
P:w21 K:w21:0:s P:w21 K:w21:1:v P:w21 K:w21:2:s P:w21 K:w21:3:s M:11 S:11 I:11 Q:w20 Q:w21 H:w21 R:11
A:10 P:w30 K:w30:0:s P:w30 K:w30:1:s M:12 S:12 I:12 R:12 A:11 P:w30 K:w30:2:s P:w30 K:w30:3:s M:13 S:13
I:13 R:13 A:12 LW:5:b P:w31 K:w31:0:s P:w31 K:w31:1:v M:20 S:20 I:20 R:20 A:13 P:w31 K:w31:2:s P:w31
K:w31:3:s M:21 S:21 I:21 Q:w30 Q:w31 H:w31 R:21 A:20 P:w40 K:w40:0:s P:w40 K:w40:1:s M:22 S:22 I:22 R:22
A:21 P:w40 K:w40:2:s P:w40 K:w40:3:s M:23 S:23 I:23 R:23 A:22 P:w41 K:w41:0:s P:w41 K:w41:1:v M:30 S:30
I:30 R:30 A:23 P:w41 K:w41:2:s P:w41 K:w41:3:s M:31 S:31 I:31 Q:w40 Q:w41 H:w41 R:31 A:30 P:w50 K:w50:0:s
P:w50 K:w50:1:s M:32 S:32 I:32 R:32 A:31 P:w50 K:w50:2:s P:w50 K:w50:3:s M:33 S:33 I:33 R:33 A:32 P:w51
K:w51:0:s P:w51 K:w51:1:v M:40 S:40 I:40 R:40 A:33 P:w51 K:w51:2:s P:w51 K:w51:3:s M:41 S:41 I:41 Q:w50
Q:w51 H:w51 R:41 A:40 M:42 S:42 I:42 R:42 A:41 M:43 S:43 I:43 M:50 C:0 R:43 A:42:v M:51 C:1 M:52 C:2
A:43:v M:53 C:3
"""


def tile_attention_pa_kernel(tc, x, freqs_cis, wqkv, q_norm_w, k_norm_w, out_0, out_1, out_2):
    nc = tc.nc
    with ExitStack() as ctx:
        const = ctx.enter_context(tc.tile_pool(name="const", bufs=1))
        w_pool = ctx.enter_context(tc.tile_pool(name="w_pool", bufs=3))
        stage = ctx.enter_context(tc.tile_pool(name="stage", bufs=3))
        x_stage = ctx.enter_context(tc.tile_pool(name="x_stage", bufs=3))
        head_stage = ctx.enter_context(tc.tile_pool(name="head_stage", bufs=8))
        quantised = ctx.enter_context(tc.tile_pool(name="quantised", bufs=5))
        work = ctx.enter_context(tc.tile_pool(name="work", bufs=14))
        results = ctx.enter_context(tc.tile_pool(name="results", bufs=4))
        small = ctx.enter_context(tc.tile_pool(name="small", bufs=4))
        norms = ctx.enter_context(tc.tile_pool(name="norms", bufs=20))
        t_psum = ctx.enter_context(tc.psum_pool(name="t_psum", bufs=4))
        acc_psum = ctx.enter_context(tc.psum_pool(name="acc_psum", bufs=8 - 4))
        ctx.enter_context(tc.manual_schedule())

        x_rows_dram = x.rearrange("b s k -> (b s) k")
        out_dram = [
            out_0.rearrange("b s h d -> (b s) (h d)"),
            out_1.rearrange("b s h d -> (b s) (h d)"),
            out_2.rearrange("b s h d -> (b s) (h d)"),
        ]

        gain_row = const.tile([P, 2, HD], BF16, name="gain_row")
        freqs = const.tile([P, 2, HP, 2], BF16, name="freqs")
        x_rows = const.tile([P, TOKEN_TILES, D], BF16, name="x_rows")
        eps = const.tile([P, 1], F32, name="eps")
        warm = const.tile([P, 1], F32, name="warm")
        ones = const.tile([P, P], BF16, name="ones")
        ident = const.tile([P, P], F32, name="ident")
        gains = const.tile([P, 2, HP, 2], F32, name="gains")
        w_rows = {}

        def load_x(m):
            nc.sync.dma_start(out=x_rows[:, m, :], in_=x_rows_dram[P * m : P * (m + 1), :])

        def load_w(g, how):
            w_rows[g] = w_pool.tile([P, HEADS, D], BF16, name="w_rows")
            per, parts = {"h": (1, 1), "q": (2, 2), "b": (2, 1), "p": (4, 2)}[how]
            for b in range(HEADS // per):
                first = GROUP * g + P * per * b
                w = D // parts
                for i in range(parts):
                    nc.sync.dma_start(
                        out=w_rows[g][:, per * b : per * (b + 1), w * i : w * (i + 1)],
                        in_=wqkv[first : first + P * per, w * i : w * (i + 1)].rearrange("(h p) k -> p h k", p=P),
                    )

        def load_head(h):
            if 0 not in w_rows:
                w_rows[0] = w_pool.tile([P, HEADS, D], BF16, name="w_rows")
            nc.sync.dma_start(out=w_rows[0][:, h, :], in_=wqkv[P * h : P * (h + 1), :])

        def load_small(queue):
            queue.dma_start(out=gain_row[0:1, 0, :], in_=q_norm_w.unsqueeze(0))
            queue.dma_start(out=gain_row[0:1, 1, :], in_=k_norm_w.unsqueeze(0))
            queue.dma_start(out=freqs[:], in_=freqs_cis.rearrange("(a p) j t -> p a j t", p=P))

        def spread_gains():
            gain_bank = t_psum.tile([P, 2, HALF], F32, name="bank")
            nc.tensor.matmul(
                out=gain_bank[:, 0, :], lhsT=ones[:], rhs=gain_row[:].rearrange("p a d -> p (a d)"), start=True, stop=True
            )
            nc.scalar.copy(out=gains[:].rearrange("p a j e -> p (a j e)"), in_=gain_bank[:, 0, :])

        factors = {}

        def make_factors(kind, a):
            table = const.tile([P, 2, HP, 2], F32, name="factors%d%d" % (kind, a))
            nc.vector.tensor_tensor(
                out=table[:, 0, :, :],
                in0=gains[:, kind, :, :],
                in1=freqs[:, a, :, 0].unsqueeze(2).to_broadcast([P, HP, 2]),
                op=ALU.mult,
            )
            nc.vector.tensor_tensor(
                out=table[:, 1, :, 0], in0=gains[:, kind, :, 0], in1=freqs[:, a, :, 1], op=ALU.mult
            )
            nc.vector.scalar_tensor_tensor(
                out=table[:, 1, :, 1],
                in0=gains[:, kind, :, 1],
                scalar=-1.0,
                in1=freqs[:, a, :, 1],
                op0=ALU.mult,
                op1=ALU.mult,
            )
            factors[(kind, a)] = table

        x_codes = const.tile([P, TOKEN_TILES, PASSES * P], U32, align_bytes=64, name="x_codes")
        x_scales = const.tile([P, TOKEN_TILES, PASSES * P], U8, align_bytes=64, name="x_scales")
        operand = {}
        units = {}

        def new_unit(name):
            kind = name[0]
            if kind == "x":
                m = int(name[1])
                pieces = [(x_rows[:, m, :], c) for c in range(PASSES)]
                codes, scales = x_codes[:, m, :], x_scales[:, m, :]
            elif kind == "w":
                g, half = int(name[1]), int(name[2])
                ct = quantised.tile([P, 2, GROUP], U32, align_bytes=64, name="w_codes")
                st = quantised.tile([P, 2, GROUP], U8, align_bytes=64, name="w_scales")
                operand[name] = (ct, st)
                pieces = [(w_rows[g][:, h, :], 2 * half + i) for i in range(2) for h in range(HEADS)]
                codes, scales = ct[:].rearrange("p c n -> p (c n)"), st[:].rearrange("p c n -> p (c n)")
            elif kind == "h":
                b = int(name[1])
                ct = quantised.tile([P, PASSES, HALF], U32, align_bytes=64, name="w_codes")
                st = quantised.tile([P, PASSES, HALF], U8, align_bytes=64, name="w_scales")
                operand[name] = (ct, st)
                pieces = [(w_rows[0][:, 2 * b + i, :], c) for c in range(PASSES) for i in range(2)]
                codes, scales = ct[:].rearrange("p c n -> p (c n)"), st[:].rearrange("p c n -> p (c n)")
            elif kind == "k":
                h = int(name[1])
                ct = const.tile([P, PASSES, HD], U32, align_bytes=64, name="k_codes%d" % h)
                st = const.tile([P, PASSES, HD], U8, align_bytes=64, name="k_scales%d" % h)
                operand[name] = (ct, st)
                pieces = [(w_rows[0][:, h, :], c) for c in range(PASSES)]
                codes, scales = ct[:].rearrange("p c n -> p (c n)"), st[:].rearrange("p c n -> p (c n)")
            else:
                c, b = int(name[1]), int(name[2])
                whole = "w0%d" % (c // 2)
                if whole not in operand:
                    operand[whole] = (
                        quantised.tile([P, 2, GROUP], U32, align_bytes=64, name="w_codes"),
                        quantised.tile([P, 2, GROUP], U8, align_bytes=64, name="w_scales"),
                    )
                ct, st = operand[whole]
                pieces = [(w_rows[0][:, 2 * b + i, :], c) for i in range(2)]
                codes = ct[:, c % 2, HALF * b : HALF * (b + 1)]
                scales = st[:, c % 2, HALF * b : HALF * (b + 1)]
            banks = len(pieces) // 2
            grouped = {4: stage, 2: x_stage, 1: head_stage}[banks].tile(
                [P, banks * HALF, PACK], BF16, align_bytes=64, name="grouped%d" % banks
            )
            units[name] = [pieces, codes, scales, grouped, []]

        def turn_bank(name):
            if name not in units:
                new_unit(name)
            unit = units[name]
            n = len(unit[4])
            bank = t_psum.tile([P, 2, HALF], F32, name="bank")
            unit[4].append(bank)
            for u in range(2):
                for i in range(2):
                    rows, c = unit[0][2 * n + i]
                    first = WORDS_PASS * c + P * u
                    nc.tensor.transpose(
                        out=bank[:, u, P * i : P * (i + 1)],
                        in_=rows.bitcast(F32)[:, first : first + P],
                        identity=ident[:],
                    )
            return n

        def copy_bank(name, n, on_vector):
            unit = units[name]
            dst = unit[3][:].bitcast(F32)[:, HALF * n : HALF * (n + 1), :]
            src = unit[4][n][:].rearrange("p u n -> p n u")
            if on_vector:
                nc.vector.tensor_copy(out=dst, in_=src)
            else:
                nc.scalar.copy(out=dst, in_=src)

        def turn(name, spec):
            for letter in spec:
                n = turn_bank(name)
                copy_bank(name, n, letter in "vV")

        def quantise(name):
            pieces, codes, scales, grouped, banks = units[name]
            nc.vector.quantize_mx(out=codes.bitcast(FP8X4), scales=scales, in_=grouped[:].rearrange("p n t -> p (n t)"))

        def hold(name):
            held = small.tile([P, 1], U32, name="held")
            nc.gpsimd.tensor_copy(out=held[:], in_=units[name][1][:, 0:1])

        accs = {}
        sums = {}
        invs = {}
        prods = {}

        def product_half(m, b):
            acc = t_psum.tile([P, 2, HALF], F32, name="bank")
            accs[(V_GROUP, m, b)] = acc
            for c in range(PASSES):
                codes, scales = operand["w%d%d" % (V_GROUP, c // 2)]
                nc.tensor.matmul_mx(
                    out=acc[:, 0, :],
                    lhsT=x_codes[:, m, P * c : P * (c + 1)].bitcast(FP8X4),
                    lhsT_scale=x_scales[:, m, P * c : P * (c + 1)],
                    rhs=codes[:, c % 2, HALF * b : HALF * (b + 1)].bitcast(FP8X4),
                    rhs_scale=scales[:, c % 2, HALF * b : HALF * (b + 1)],
                    start=(c == 0),
                    stop=(c == PASSES - 1),
                )

        def copy_half(m, b, engine_copy):
            half_result = results.tile([P, HALF], F32, name="half_result")
            engine_copy(out=half_result[:], in_=accs[(V_GROUP, m, b)][:, 0, :])
            nc.sync.dma_start(out=out_dram[2][P * m : P * (m + 1), HALF * b : HALF * (b + 1)], in_=half_result[:])

        def product(g, m, part):
            if (g, m) not in accs:
                if g == V_GROUP:
                    acc = t_psum.tile([P, 2, HALF], F32, name="bank")
                    accs[(g, m)] = (acc, acc[:].rearrange("p u n -> p (u n)"))
                else:
                    acc = acc_psum.tile([P, HEADS, HD], F32, name="acc")
                    accs[(g, m)] = (acc, acc[:].rearrange("p h d -> p (h d)"))
            flat = accs[(g, m)][1]
            passes = {"a": (0, 1), "b": (2, 3)}.get(part, range(PASSES))
            part = "" if part in ("a", "b") else part
            for c in passes:
                if part:
                    codes, scales = operand[part]
                    width = HALF if part[0] == "h" else HD
                    at = width * int(part[1])
                    rhs, rhs_scale = codes[:, c, :], scales[:, c, :]
                else:
                    codes, scales = operand["w%d%d" % (g, c // 2)]
                    at, width = 0, GROUP
                    rhs, rhs_scale = codes[:, c % 2, :], scales[:, c % 2, :]
                nc.tensor.matmul_mx(
                    out=flat[:, at : at + width],
                    lhsT=x_codes[:, m, P * c : P * (c + 1)].bitcast(FP8X4),
                    lhsT_scale=x_scales[:, m, P * c : P * (c + 1)],
                    rhs=rhs.bitcast(FP8X4),
                    rhs_scale=rhs_scale,
                    start=(c == 0),
                    stop=(c == PASSES - 1),
                )

        def squares_of(g, m, heads):
            acc = accs[(g, m)][0]
            if (g, m) not in sums:
                sums[(g, m)] = norms.tile([P, HEADS], F32, name="sumsq")
            sumsq = sums[(g, m)]
            for h in heads:
                squares = small.tile([P, HD], BF16, name="squares")
                nc.scalar.activation(out=squares[:], in_=acc[:, h, :], func=ACT.Square, accum_out=sumsq[:, h : h + 1])

        def inverse(g, m):
            inv = norms.tile([P, HEADS], F32, name="inv")
            nc.scalar.activation(
                out=inv[:], in_=sums[(g, m)][:], func=ACT.Abs_reciprocal_sqrt, bias=eps[:, 0:1], scale=1.0 / HD
            )
            invs[(g, m)] = inv

        def rotate(g, m, heads):
            acc = accs[(g, m)][0]
            inv = invs[(g, m)]
            table = factors[(0 if g < Q_GROUPS else 1, m % 2)]
            if (g, m) not in prods:
                prods[(g, m)] = work.tile([P, 2, HEADS * HP, 2], F32, name="products")
            products = prods[(g, m)]
            for h in heads:
                nc.vector.scalar_tensor_tensor(
                    out=products[:, :, HP * h : HP * (h + 1), :].rearrange("p k j e -> p k (j e)"),
                    in0=acc[:, h, :].unsqueeze(1).to_broadcast([P, 2, HD]),
                    scalar=inv[:, h : h + 1],
                    in1=table[:].rearrange("p k j e -> p k (j e)"),
                    op0=ALU.mult,
                    op1=ALU.mult,
                )

        pending = {}

        def store(g, m, result):
            if g < Q_GROUPS:
                dst = out_dram[0][P * m : P * (m + 1), GROUP * g : GROUP * (g + 1)]
            elif g == K_GROUP:
                dst = out_dram[1][P * m : P * (m + 1), :]
            else:
                dst = out_dram[2][P * m : P * (m + 1), :]
            nc.sync.dma_start(out=dst, in_=result)

        def add(g, m, engine, later):
            products = prods[(g, m)]
            result = products[:, 0, :, :]
            engine.tensor_tensor(out=result, in0=result, in1=products[:, 1, :, ::-1], op=ALU.add)
            if later:
                pending[(g, m)] = result.rearrange("p n e -> p (n e)")
            else:
                store(g, m, result.rearrange("p n e -> p (n e)"))

        def copy_v(m, engine_copy, later):
            v_result = results.tile([P, GROUP], F32, name="result")
            engine_copy(out=v_result[:], in_=accs[(V_GROUP, m)][1])
            if later:
                pending[(V_GROUP, m)] = v_result[:]
            else:
                store(V_GROUP, m, v_result[:])

        nc.vector.memset(gain_row[:], 0.0)
        nc.vector.memset(eps[:], EPS)
        nc.vector.memset(ones[:], 1.0)
        make_identity(nc, ident[:])

        def warm_table():
            nc.scalar.activation(out=warm[:], in_=eps[:], func=ACT.Abs_reciprocal_sqrt)

        if "LS:a" not in PROGRAM:
            warm_table()

        for token in PROGRAM.split():
            part = token.split(":")
            op = part[0]
            arg = part[1] if len(part) > 1 else ""
            extra = part[2] if len(part) > 2 else ""
            if op == "LX":
                load_x(int(arg))
            elif op == "LW":
                load_w(int(arg), extra)
            elif op == "LS":
                load_small(nc.scalar if arg == "a" else nc.sync)
                if arg == "a":
                    warm_table()
            elif op == "G":
                spread_gains()
            elif op == "F":
                make_factors(int(arg[0]), int(arg[1]))
            elif op == "T":
                turn(arg, extra)
            elif op == "P":
                turn_bank(arg)
            elif op == "K":
                copy_bank(arg, int(extra), part[3] == "v")
            elif op == "Q":
                quantise(arg)
            elif op == "H":
                hold(arg)
            elif op == "M":
                product(int(arg[0]), int(arg[1]), extra)
            elif op == "S":
                squares_of(int(arg[0]), int(arg[1]), [int(h) for h in (extra or "0123")])
            elif op == "I":
                inverse(int(arg[0]), int(arg[1]))
            elif op == "R":
                rotate(int(arg[0]), int(arg[1]), [int(h) for h in (extra or "0123")])
            elif op == "A":
                add(int(arg[0]), int(arg[1]), nc.vector if "v" in extra else nc.gpsimd, "l" in extra)
            elif op == "C":
                copy_v(int(arg), nc.vector.tensor_copy if "v" in extra else nc.scalar.copy, "l" in extra)
            elif op == "MH":
                product_half(int(arg[0]), int(arg[1]))
            elif op == "CH":
                copy_half(int(arg[0]), int(arg[1]), nc.vector.tensor_copy if "v" in extra else nc.scalar.copy)
            elif op == "LH":
                load_head(int(arg))
            elif op == "O":
                store(int(arg[0]), int(arg[1]), pending[(int(arg[0]), int(arg[1]))])
            else:
                raise ValueError(token)
